import numpy as np
import ml_dtypes

BF16 = ml_dtypes.bfloat16


def bf(x):
    return np.asarray(x, np.float32).astype(BF16)


def f32(x):
    return np.asarray(x, np.float32)


def f64(x):
    return np.asarray(x).astype(np.float64)


def striped(idx):
    return np.tile(idx.reshape(-1, 16).T, (8, 1))


C, S, N, H, K = 256, 1024, 256, 128, 8


def setup_inputs():
    return {"x": f32(np.abs(np.random.standard_normal((C, S)))), "theta": f32(np.random.uniform(-1.5, 1.5, (1, K * H))), "offs": striped(np.random.permutation(S)[:N])}


def reference(x, theta, offs):
    idx = offs[:16].T.reshape(-1)
    h = f64(x)[:, idx]
    th_all = f64(theta).reshape(K, H)
    for s in range(K):
        d = 1 << s
        th = th_all[s].reshape(H // d, d)
        hr = h.reshape(C, H // d, 2, d)
        a, b = hr[:, :, 0, :], hr[:, :, 1, :]
        c, sn = np.cos(th), np.sin(th)
        h = np.stack([c * a - sn * b, sn * a + c * b], axis=2).reshape(C, N)
    return np.maximum(h, 0.0)

@@ -1,0 +1,82 @@
+import math
+
+import concourse.mybir as mybir
+
+F32 = mybir.dt.float32
+U16 = mybir.dt.uint16
+MULT = mybir.AluOpType.mult
+ADD = mybir.AluOpType.add
+SIN = mybir.ActivationFunctionType.Sin
+
+P = 128
+SAMPLES, UNITS, PICKED, ANGLES, STAGES = 256, 1024, 256, 128, 8
+BLOCKS = SAMPLES // P
+
+SIN_ROW, COS_ROW, NEG_SIN_ROW = 0, 1, 2
+
+
+def tile_quantumautoencoder_kernel(tc, x, theta, offs, out):
+    nc = tc.nc
+    with tc.tile_pool(name="held", bufs=1) as held, tc.tile_pool(name="work", bufs=2) as work:
+        offsets = held.tile([P, PICKED // 16], U16, name="offsets")
+        nc.sync.dma_start(offsets[:], offs)
+
+        angles = held.tile([P, STAGES * ANGLES], F32, name="angles")
+        nc.scalar.dma_start(angles[:], theta.to_broadcast([P, STAGES * ANGLES]))
+
+        windows = []
+        for b in range(BLOCKS):
+            window = held.tile([P, UNITS], F32, name=f"window{b}")
+            nc.sync.dma_start(window[:], x[b * P : (b + 1) * P, :])
+            windows.append(window)
+
+        half_pi = held.tile([P, 1], F32, name="half_pi")
+        nc.vector.memset(half_pi[:], math.pi / 2)
+        trig = held.tile([P, 3, STAGES * ANGLES], F32, name="trig")
+        nc.scalar.activation(trig[:, SIN_ROW, :], angles[:], SIN)
+        nc.scalar.activation(trig[:, COS_ROW, :], angles[:], SIN, bias=half_pi[:])
+        nc.scalar.activation(trig[:, NEG_SIN_ROW, :], angles[:], SIN, scale=-1.0)
+
+        first_factors = held.tile([P, 2, PICKED], F32, name="first_factors")
+        for row, first in ((0, COS_ROW), (1, SIN_ROW)):
+            nc.vector.tensor_copy(
+                first_factors[:, row, :].rearrange("p (g t) -> p g t", t=2),
+                trig[:, first : first + 2, 0:ANGLES].rearrange("p t g -> p g t"),
+            )
+
+        hidden = [None] * BLOCKS
+        for s in range(STAGES):
+            d = 1 << s
+            stage = slice(s * ANGLES, (s + 1) * ANGLES)
+            for b in range(BLOCKS):
+                products = work.tile([P, 2, PICKED], F32, name=f"products{b}")
+                for row, first in ((0, COS_ROW), (1, SIN_ROW)):
+                    if s == 0:
+                        nc.vector.tensor_tensor(
+                            products[:, row, :],
+                            windows[b][:].indirect(offsets[:]),
+                            first_factors[:, row, :],
+                            MULT,
+                        )
+                    else:
+                        factors = trig[:, first : first + 2, stage].rearrange("p t (g e) -> p g t e", e=d)
+                        nc.vector.tensor_tensor(
+                            products[:, row, :].rearrange("p (g t e) -> p g t e", t=2, e=d),
+                            hidden[b][:].rearrange("p (g t e) -> p g t e", t=2, e=d),
+                            factors,
+                            MULT,
+                        )
+                halves = products[:].rearrange("p r (g t e) -> p g r t e", t=2, e=d)
+                rotated = work.tile([P, PICKED], F32, name=f"rotated{b}")
+                nc.vector.tensor_tensor(
+                    rotated[:].rearrange("p (g r e) -> p g r e", r=2, e=d),
+                    halves[:, :, :, 0, :],
+                    halves[:, :, :, 1, :],
+                    ADD,
+                )
+                hidden[b] = rotated
+
+        for b in range(BLOCKS):
+            result = work.tile([P, PICKED], F32, name=f"result{b}")
+            nc.vector.tensor_scalar_max(result[:], hidden[b][:], 0.0)
+            nc.sync.dma_start(out[b * P : (b + 1) * P, :], result[:])

@@ -1,23 +1,56 @@
 import math
 
 import concourse.mybir as mybir
+from concourse.masks import make_identity
 
 F32 = mybir.dt.float32
 U16 = mybir.dt.uint16
 MULT = mybir.AluOpType.mult
 ADD = mybir.AluOpType.add
 SIN = mybir.ActivationFunctionType.Sin
+RELU = mybir.ActivationFunctionType.Relu
 
 P = 128
 SAMPLES, UNITS, PICKED, ANGLES, STAGES = 256, 1024, 256, 128, 8
 BLOCKS = SAMPLES // P
+HALVES = PICKED // P
+
+FLOPS = SAMPLES * STAGES * ANGLES * 6
 
 SIN_ROW, COS_ROW, NEG_SIN_ROW = 0, 1, 2
+FIRST_ROWS = (COS_ROW, SIN_ROW)
+
+
+def fill_trig(nc, trig, angles, half_pi, s):
+    stage = slice(s * ANGLES, (s + 1) * ANGLES)
+    nc.scalar.activation(trig[:, SIN_ROW, stage], angles[:, stage], SIN)
+    nc.scalar.activation(trig[:, COS_ROW, stage], angles[:, stage], SIN, bias=half_pi[:])
+    nc.scalar.activation(trig[:, NEG_SIN_ROW, stage], angles[:, stage], SIN, scale=-1.0)
+
+
+def factors(trig, row, s):
+    first = FIRST_ROWS[row]
+    stage = slice(s * ANGLES, (s + 1) * ANGLES)
+    return trig[:, first : first + 2, stage].rearrange("p t (g e) -> p g t e", e=1 << s)
+
+
+def add_halves(nc, new, products, s):
+    halves = products[:].rearrange("p r (g t e) -> p g r t e", t=2, e=1 << s)
+    nc.vector.tensor_tensor(
+        new[:].rearrange("p (g r e) -> p g r e", r=2, e=1 << s),
+        halves[:, :, :, 0, :],
+        halves[:, :, :, 1, :],
+        ADD,
+    )
 
 
 def tile_quantumautoencoder_kernel(tc, x, theta, offs, out):
     nc = tc.nc
-    with tc.tile_pool(name="held", bufs=1) as held, tc.tile_pool(name="work", bufs=2) as work:
+    with (
+        tc.tile_pool(name="held", bufs=1) as held,
+        tc.tile_pool(name="work", bufs=2) as work,
+        tc.psum_pool(name="psum", bufs=1) as psum,
+    ):
         offsets = held.tile([P, PICKED // 16], U16, name="offsets")
         nc.sync.dma_start(offsets[:], offs)
 
@@ -32,51 +65,59 @@ def tile_quantumautoencoder_kernel(tc, x, theta, offs, out):
 
         half_pi = held.tile([P, 1], F32, name="half_pi")
         nc.vector.memset(half_pi[:], math.pi / 2)
+        eyes = held.tile([P, PICKED], F32, name="eyes")
+        for t in range(HALVES):
+            make_identity(nc, eyes[:, t * P : (t + 1) * P])
         trig = held.tile([P, 3, STAGES * ANGLES], F32, name="trig")
-        nc.scalar.activation(trig[:, SIN_ROW, :], angles[:], SIN)
-        nc.scalar.activation(trig[:, COS_ROW, :], angles[:], SIN, bias=half_pi[:])
-        nc.scalar.activation(trig[:, NEG_SIN_ROW, :], angles[:], SIN, scale=-1.0)
 
+        fill_trig(nc, trig, angles, half_pi, 0)
         first_factors = held.tile([P, 2, PICKED], F32, name="first_factors")
-        for row, first in ((0, COS_ROW), (1, SIN_ROW)):
-            nc.vector.tensor_copy(
-                first_factors[:, row, :].rearrange("p (g t) -> p g t", t=2),
-                trig[:, first : first + 2, 0:ANGLES].rearrange("p t g -> p g t"),
+        for row in range(2):
+            nc.gpsimd.tensor_copy(
+                first_factors[:, row, :].rearrange("p (g t e) -> p g t e", t=2, e=1), factors(trig, row, 0)
             )
-
-        hidden = [None] * BLOCKS
-        for s in range(STAGES):
-            d = 1 << s
-            stage = slice(s * ANGLES, (s + 1) * ANGLES)
-            for b in range(BLOCKS):
-                products = work.tile([P, 2, PICKED], F32, name=f"products{b}")
-                for row, first in ((0, COS_ROW), (1, SIN_ROW)):
-                    if s == 0:
-                        nc.vector.tensor_tensor(
-                            products[:, row, :],
-                            windows[b][:].indirect(offsets[:]),
-                            first_factors[:, row, :],
-                            MULT,
-                        )
-                    else:
-                        factors = trig[:, first : first + 2, stage].rearrange("p t (g e) -> p g t e", e=d)
-                        nc.vector.tensor_tensor(
-                            products[:, row, :].rearrange("p (g t e) -> p g t e", t=2, e=d),
-                            hidden[b][:].rearrange("p (g t e) -> p g t e", t=2, e=d),
-                            factors,
-                            MULT,
-                        )
-                halves = products[:].rearrange("p r (g t e) -> p g r t e", t=2, e=d)
-                rotated = work.tile([P, PICKED], F32, name=f"rotated{b}")
-                nc.vector.tensor_tensor(
-                    rotated[:].rearrange("p (g r e) -> p g r e", r=2, e=d),
-                    halves[:, :, :, 0, :],
-                    halves[:, :, :, 1, :],
-                    ADD,
-                )
-                hidden[b] = rotated
-
+        flipped = []
         for b in range(BLOCKS):
-            result = work.tile([P, PICKED], F32, name=f"result{b}")
-            nc.vector.tensor_scalar_max(result[:], hidden[b][:], 0.0)
+            products = work.tile([P, 2, PICKED], F32, name="sample_products")
+            for row in range(2):
+                nc.vector.tensor_tensor(
+                    products[:, row, :], windows[b][:].indirect(offsets[:]), first_factors[:, row, :], MULT
+                )
+            rotated = work.tile([P, PICKED], F32, name="sample_rotated")
+            add_halves(nc, rotated, products, 0)
+            flipped_psum = psum.tile([P, HALVES, P], F32, name=f"flipped_psum{b}")
+            for t in range(HALVES):
+                nc.tensor.transpose(flipped_psum[:, t, :], rotated[:, t * P : (t + 1) * P], eyes[:, 0:P])
+            flipped_b = held.tile([P, HALVES, P], F32, name=f"flipped{b}")
+            nc.scalar.copy(flipped_b[:], flipped_psum[:])
+            flipped.append(flipped_b)
+
+        matrix = eyes
+        for s in range(1, STAGES):
+            fill_trig(nc, trig, angles, half_pi, s)
+            products = work.tile([P, 2, PICKED], F32, name="matrix_products")
+            for row in range(2):
+                nc.vector.tensor_tensor(
+                    products[:, row, :].rearrange("p (g t e) -> p g t e", t=2, e=1 << s),
+                    matrix[:].rearrange("p (g t e) -> p g t e", t=2, e=1 << s),
+                    factors(trig, row, s),
+                    MULT,
+                )
+            if s < STAGES - 1:
+                matrix = work.tile([P, PICKED], F32, name="matrix")
+                add_halves(nc, matrix, products, s)
+
+        last = products[:].rearrange("p r (t e) -> p t r e", t=HALVES)
+        for b in range(BLOCKS):
+            out_psum = psum.tile([P, PICKED], F32, name=f"out_psum{b}")
+            for t in range(HALVES):
+                nc.tensor.matmul(
+                    out_psum[:].rearrange("p (r e) -> p r e", r=2),
+                    flipped[b][:, t, :],
+                    last[:, t, :, :],
+                    start=(t == 0),
+                    stop=(t == HALVES - 1),
+                )
+            result = work.tile([P, PICKED], F32, name="result")
+            nc.scalar.activation(result[:], out_psum[:], RELU)
             nc.sync.dma_start(out[b * P : (b + 1) * P, :], result[:])

@@ -9,11 +9,13 @@ MULT = mybir.AluOpType.mult
 ADD = mybir.AluOpType.add
 SIN = mybir.ActivationFunctionType.Sin
 RELU = mybir.ActivationFunctionType.Relu
+X_AXIS = mybir.AxisListType.X
 
 P = 128
 SAMPLES, UNITS, PICKED, ANGLES, STAGES = 256, 1024, 256, 128, 8
 BLOCKS = SAMPLES // P
 HALVES = PICKED // P
+LAST = STAGES - 1
 
 FLOPS = SAMPLES * STAGES * ANGLES * 6
 
@@ -21,27 +23,9 @@ SIN_ROW, COS_ROW, NEG_SIN_ROW = 0, 1, 2
 FIRST_ROWS = (COS_ROW, SIN_ROW)
 
 
-def fill_trig(nc, trig, angles, half_pi, s):
-    stage = slice(s * ANGLES, (s + 1) * ANGLES)
-    nc.scalar.activation(trig[:, SIN_ROW, stage], angles[:, stage], SIN)
-    nc.scalar.activation(trig[:, COS_ROW, stage], angles[:, stage], SIN, bias=half_pi[:])
-    nc.scalar.activation(trig[:, NEG_SIN_ROW, stage], angles[:, stage], SIN, scale=-1.0)
-
-
 def factors(trig, row, s):
     first = FIRST_ROWS[row]
-    stage = slice(s * ANGLES, (s + 1) * ANGLES)
-    return trig[:, first : first + 2, stage].rearrange("p t (g e) -> p g t e", e=1 << s)
-
-
-def add_halves(nc, new, products, s):
-    halves = products[:].rearrange("p r (g t e) -> p g r t e", t=2, e=1 << s)
-    nc.vector.tensor_tensor(
-        new[:].rearrange("p (g r e) -> p g r e", r=2, e=1 << s),
-        halves[:, :, :, 0, :],
-        halves[:, :, :, 1, :],
-        ADD,
-    )
+    return trig[:, first : first + 2, s * ANGLES : (s + 1) * ANGLES].rearrange("p t (g e) -> p g t e", e=1 << s)
 
 
 def tile_quantumautoencoder_kernel(tc, x, theta, offs, out):
@@ -50,73 +34,111 @@ def tile_quantumautoencoder_kernel(tc, x, theta, offs, out):
         tc.tile_pool(name="held", bufs=1) as held,
         tc.tile_pool(name="work", bufs=2) as work,
         tc.psum_pool(name="psum", bufs=1) as psum,
+        tc.psum_pool(name="ring", bufs=2) as ring,
     ):
         offsets = held.tile([P, PICKED // 16], U16, name="offsets")
         nc.sync.dma_start(offsets[:], offs)
-
-        angles = held.tile([P, STAGES * ANGLES], F32, name="angles")
-        nc.scalar.dma_start(angles[:], theta.to_broadcast([P, STAGES * ANGLES]))
-
         windows = []
         for b in range(BLOCKS):
             window = held.tile([P, UNITS], F32, name=f"window{b}")
             nc.sync.dma_start(window[:], x[b * P : (b + 1) * P, :])
             windows.append(window)
 
+        eye = held.tile([P, P], F32, name="eye")
+        make_identity(nc, eye[:])
+
         half_pi = held.tile([P, 1], F32, name="half_pi")
         nc.vector.memset(half_pi[:], math.pi / 2)
-        eyes = held.tile([P, PICKED], F32, name="eyes")
-        for t in range(HALVES):
-            make_identity(nc, eyes[:, t * P : (t + 1) * P])
+        angles = held.tile([P, STAGES * ANGLES], F32, name="angles")
         trig = held.tile([P, 3, STAGES * ANGLES], F32, name="trig")
+        for s in (0, LAST):
+            stage = slice(s * ANGLES, (s + 1) * ANGLES)
+            nc.scalar.dma_start(angles[:, stage], theta[:, stage].to_broadcast([P, ANGLES]))
+            nc.scalar.activation(trig[:, SIN_ROW, stage], angles[:, stage], SIN)
+            nc.scalar.activation(trig[:, COS_ROW, stage], angles[:, stage], SIN, bias=half_pi[:])
+            nc.scalar.activation(trig[:, NEG_SIN_ROW, stage], angles[:, stage], SIN, scale=-1.0)
 
-        fill_trig(nc, trig, angles, half_pi, 0)
+        own = held.tile([P, 2 * P], F32, name="own")
+        nc.gpsimd.memset(own[:], 0.0)
+        for s in range(1, LAST):
+            d = 1 << s
+            runs = theta[0, s * ANGLES : (s + 1) * ANGLES].rearrange("(t h e) -> h t e", t=HALVES, e=d)
+            for bit, queue in ((0, nc.scalar), (1, nc.gpsimd)):
+                rows = slice(bit * 64, bit * 64 + 64 // d)
+                queue.dma_start(own[rows, 2 * d : 4 * d].rearrange("k (t e) -> k t e", t=HALVES), runs)
+        phase = held.tile([P, 2], F32, name="phase")
+        nc.vector.memset(phase[:], 0.0)
+        nc.vector.memset(phase[0:64, 0:1], math.pi / 2)
+        nc.vector.memset(phase[64:128, 1:2], math.pi / 2)
+        coef = held.tile([P, 2, 2 * P], F32, name="coef")
+        nc.scalar.activation(coef[:, 0, :], own[:], SIN, bias=phase[:, 0:1], scale=-1.0)
+        nc.scalar.activation(coef[:, 1, :], own[:], SIN, bias=phase[:, 1:2])
+
+        seeds = work.tile([P, HALVES, 2], F32, name="paths")
+        nc.vector.reduce_sum(
+            seeds[:],
+            eye[:].rearrange("p (h j) -> p j h", j=2).unsqueeze(1).to_broadcast([P, HALVES, 2, P // 2]),
+            axis=X_AXIS,
+        )
+        paths = seeds[:]
+        for s in range(1, LAST):
+            d = 1 << s
+            spread = held.tile([P, P], F32, name=f"spread{s}")
+            nc.vector.tensor_copy(
+                spread[:].rearrange("k (h b e) -> k h b e", b=2, e=d),
+                eye[:].rearrange("k (b h) -> k h b", b=2)[:, 0 : 64 // d, :].unsqueeze(3).to_broadcast([P, 64 // d, 2, d]),
+            )
+            steps = ring.tile([P, 2, HALVES, d], F32, name="steps")
+            nc.tensor.matmul(steps[:], spread[:], coef[:, :, 2 * d : 4 * d])
+            longer = work.tile([P, HALVES, 2, d], F32, name="paths")
+            nc.vector.tensor_tensor(
+                longer[:],
+                paths.unsqueeze(2).to_broadcast([P, HALVES, 2, d]),
+                steps[:].rearrange("p b t e -> p t b e"),
+                MULT,
+            )
+            paths = longer[:].rearrange("p t b e -> p t (b e)")
+
+        last = held.tile([P, 2, PICKED], F32, name="last")
+        for row in range(2):
+            nc.vector.tensor_tensor(
+                last[:, row, :].rearrange("p (g t e) -> p g t e", t=2, e=P),
+                paths.unsqueeze(1),
+                factors(trig, row, LAST),
+                MULT,
+            )
+
         first_factors = held.tile([P, 2, PICKED], F32, name="first_factors")
         for row in range(2):
             nc.gpsimd.tensor_copy(
                 first_factors[:, row, :].rearrange("p (g t e) -> p g t e", t=2, e=1), factors(trig, row, 0)
             )
-        flipped = []
         for b in range(BLOCKS):
-            products = work.tile([P, 2, PICKED], F32, name="sample_products")
+            products = work.tile([P, 2, PICKED], F32, name="products")
             for row in range(2):
                 nc.vector.tensor_tensor(
                     products[:, row, :], windows[b][:].indirect(offsets[:]), first_factors[:, row, :], MULT
                 )
-            rotated = work.tile([P, PICKED], F32, name="sample_rotated")
-            add_halves(nc, rotated, products, 0)
+            sides = products[:].rearrange("p r (g t) -> p g r t", t=2)
+            rotated = work.tile([P, PICKED], F32, name="rotated")
+            nc.vector.tensor_tensor(
+                rotated[:].rearrange("p (g r) -> p g r", r=2), sides[:, :, :, 0], sides[:, :, :, 1], ADD
+            )
+
             flipped_psum = psum.tile([P, HALVES, P], F32, name=f"flipped_psum{b}")
-            for t in range(HALVES):
-                nc.tensor.transpose(flipped_psum[:, t, :], rotated[:, t * P : (t + 1) * P], eyes[:, 0:P])
-            flipped_b = held.tile([P, HALVES, P], F32, name=f"flipped{b}")
-            nc.scalar.copy(flipped_b[:], flipped_psum[:])
-            flipped.append(flipped_b)
+            for half in range(HALVES):
+                nc.tensor.transpose(flipped_psum[:, half, :], rotated[:, half * P : (half + 1) * P], eye[:])
+            flipped = work.tile([P, HALVES, P], F32, name="flipped")
+            nc.scalar.copy(flipped[:], flipped_psum[:])
 
-        matrix = eyes
-        for s in range(1, STAGES):
-            fill_trig(nc, trig, angles, half_pi, s)
-            products = work.tile([P, 2, PICKED], F32, name="matrix_products")
-            for row in range(2):
-                nc.vector.tensor_tensor(
-                    products[:, row, :].rearrange("p (g t e) -> p g t e", t=2, e=1 << s),
-                    matrix[:].rearrange("p (g t e) -> p g t e", t=2, e=1 << s),
-                    factors(trig, row, s),
-                    MULT,
-                )
-            if s < STAGES - 1:
-                matrix = work.tile([P, PICKED], F32, name="matrix")
-                add_halves(nc, matrix, products, s)
-
-        last = products[:].rearrange("p r (t e) -> p t r e", t=HALVES)
-        for b in range(BLOCKS):
             out_psum = psum.tile([P, PICKED], F32, name=f"out_psum{b}")
-            for t in range(HALVES):
+            for half in range(HALVES):
                 nc.tensor.matmul(
-                    out_psum[:].rearrange("p (r e) -> p r e", r=2),
-                    flipped[b][:, t, :],
-                    last[:, t, :, :],
-                    start=(t == 0),
-                    stop=(t == HALVES - 1),
+                    out_psum[:],
+                    flipped[:, half, :],
+                    last[:].rearrange("p r (t e) -> p t r e", t=HALVES)[:, half, :, :],
+                    start=(half == 0),
+                    stop=(half == HALVES - 1),
                 )
             result = work.tile([P, PICKED], F32, name="result")
             nc.scalar.activation(result[:], out_psum[:], RELU)

@@ -4,38 +4,33 @@ import concourse.mybir as mybir
 from concourse.masks import make_identity
 
 F32 = mybir.dt.float32
+I32 = mybir.dt.int32
 U16 = mybir.dt.uint16
 MULT = mybir.AluOpType.mult
 ADD = mybir.AluOpType.add
+SHIFT_RIGHT = mybir.AluOpType.logical_shift_right
+AND = mybir.AluOpType.bitwise_and
 SIN = mybir.ActivationFunctionType.Sin
 RELU = mybir.ActivationFunctionType.Relu
-X_AXIS = mybir.AxisListType.X
 
 P = 128
 SAMPLES, UNITS, PICKED, ANGLES, STAGES = 256, 1024, 256, 128, 8
 BLOCKS = SAMPLES // P
-HALVES = PICKED // P
-LAST = STAGES - 1
+PAIRS = PICKED // 2
+QUARTER_TURN = math.pi / 2
 
 FLOPS = SAMPLES * STAGES * ANGLES * 6
-
-SIN_ROW, COS_ROW, NEG_SIN_ROW = 0, 1, 2
-FIRST_ROWS = (COS_ROW, SIN_ROW)
-
-
-def factors(trig, row, s):
-    first = FIRST_ROWS[row]
-    return trig[:, first : first + 2, s * ANGLES : (s + 1) * ANGLES].rearrange("p t (g e) -> p g t e", e=1 << s)
 
 
 def tile_quantumautoencoder_kernel(tc, x, theta, offs, out):
     nc = tc.nc
     with (
         tc.tile_pool(name="held", bufs=1) as held,
-        tc.tile_pool(name="work", bufs=2) as work,
+        tc.tile_pool(name="work", bufs=BLOCKS) as work,
         tc.psum_pool(name="psum", bufs=1) as psum,
-        tc.psum_pool(name="ring", bufs=2) as ring,
     ):
+        first_angles = held.tile([P, ANGLES], F32, name="first_angles")
+        nc.sync.dma_start(first_angles[:], theta[:, 0:ANGLES].to_broadcast([P, ANGLES]))
         offsets = held.tile([P, PICKED // 16], U16, name="offsets")
         nc.sync.dma_start(offsets[:], offs)
         windows = []
@@ -44,102 +39,115 @@ def tile_quantumautoencoder_kernel(tc, x, theta, offs, out):
             nc.sync.dma_start(window[:], x[b * P : (b + 1) * P, :])
             windows.append(window)
 
+        table = held.tile([P, 2 * P], F32, name="table")
+        nc.gpsimd.memset(table[:], 0.0)
+        for s in range(1, STAGES):
+            d = 1 << s
+            runs = P // d
+            nc.scalar.dma_start(
+                table[runs : 2 * runs, d : 2 * d],
+                theta[0, s * ANGLES : (s + 1) * ANGLES].rearrange("(h e) -> h e", e=d),
+            )
+
+        quarter_turn = held.tile([P, 1], F32, name="quarter_turn")
+        nc.vector.memset(quarter_turn[:], QUARTER_TURN)
+
+        first_phase = held.tile([P, PAIRS, 2], F32, name="first_phase")
+        nc.vector.memset(first_phase[:, :, 0], 0.0)
+        nc.vector.memset(first_phase[:, :, 1], QUARTER_TURN)
+
+        row_number = held.tile([P, 1], I32, name="row_number")
+        nc.gpsimd.iota(row_number[:], pattern=[[0, 1]], base=0, channel_multiplier=1)
+        bits = held.tile([P, 2 * P], I32, name="bits")
+        for s in range(1, STAGES):
+            d = 1 << s
+            nc.vector.tensor_scalar(
+                bits[:, d : 2 * d], row_number[:].to_broadcast([P, d]), s - 1, 1, SHIFT_RIGHT, AND
+            )
+        phase = held.tile([P, 2 * P], F32, name="phase")
+        nc.vector.tensor_scalar(phase[:, 2:], bits[:, 2:], QUARTER_TURN, None, MULT)
+
+        first_turns = held.tile([P, PAIRS, 2], F32, name="first_turns")
+        nc.vector.tensor_tensor(
+            first_turns[:], first_angles[:].unsqueeze(2).to_broadcast([P, PAIRS, 2]), first_phase[:], ADD
+        )
+        first_factors = held.tile([P, 2, PICKED], F32, name="first_factors")
+        flat_first_turns = first_turns[:].rearrange("p g t -> p (g t)")
+        nc.scalar.activation(first_factors[:, 0, :], flat_first_turns, SIN, bias=quarter_turn[:], scale=-1.0)
+        nc.scalar.activation(first_factors[:, 1, :], flat_first_turns, SIN)
+
         eye = held.tile([P, P], F32, name="eye")
         make_identity(nc, eye[:])
-
-        half_pi = held.tile([P, 1], F32, name="half_pi")
-        nc.vector.memset(half_pi[:], math.pi / 2)
-        angles = held.tile([P, STAGES * ANGLES], F32, name="angles")
-        trig = held.tile([P, 3, STAGES * ANGLES], F32, name="trig")
-        for s in (0, LAST):
-            stage = slice(s * ANGLES, (s + 1) * ANGLES)
-            nc.scalar.dma_start(angles[:, stage], theta[:, stage].to_broadcast([P, ANGLES]))
-            nc.scalar.activation(trig[:, SIN_ROW, stage], angles[:, stage], SIN)
-            nc.scalar.activation(trig[:, COS_ROW, stage], angles[:, stage], SIN, bias=half_pi[:])
-            nc.scalar.activation(trig[:, NEG_SIN_ROW, stage], angles[:, stage], SIN, scale=-1.0)
-
-        own = held.tile([P, 2 * P], F32, name="own")
-        nc.gpsimd.memset(own[:], 0.0)
-        for s in range(1, LAST):
+        spread = held.tile([P, P], F32, name="spread")
+        for s in range(1, STAGES):
             d = 1 << s
-            runs = theta[0, s * ANGLES : (s + 1) * ANGLES].rearrange("(t h e) -> h t e", t=HALVES, e=d)
-            for bit, queue in ((0, nc.scalar), (1, nc.gpsimd)):
-                rows = slice(bit * 64, bit * 64 + 64 // d)
-                queue.dma_start(own[rows, 2 * d : 4 * d].rearrange("k (t e) -> k t e", t=HALVES), runs)
-        phase = held.tile([P, 2], F32, name="phase")
-        nc.vector.memset(phase[:], 0.0)
-        nc.vector.memset(phase[0:64, 0:1], math.pi / 2)
-        nc.vector.memset(phase[64:128, 1:2], math.pi / 2)
+            runs = P // d
+            takers = spread[:].rearrange("k (h e) -> k h e", e=d)
+            own_run = eye[:, runs : 2 * runs].unsqueeze(2).to_broadcast([P, runs, d])
+            if s == 1:
+                nc.gpsimd.tensor_copy(takers, own_run)
+            else:
+                nc.gpsimd.tensor_tensor(takers, takers, own_run, ADD)
+
+        turns = psum.tile([P, 2 * P], F32, name="turns")
+        nc.tensor.matmul(turns[:, 2:], eye[:], phase[:, 2:], start=True, stop=False)
+        nc.tensor.matmul(turns[:, 2:], spread[:], table[:, 2:], start=False, stop=True)
         coef = held.tile([P, 2, 2 * P], F32, name="coef")
-        nc.scalar.activation(coef[:, 0, :], own[:], SIN, bias=phase[:, 0:1], scale=-1.0)
-        nc.scalar.activation(coef[:, 1, :], own[:], SIN, bias=phase[:, 1:2])
+        nc.scalar.activation(coef[:, 1, 2:], turns[:, 2:], SIN)
+        nc.scalar.activation(coef[:, 0, 2:], turns[:, 2:], SIN, bias=quarter_turn[:], scale=-1.0)
 
-        seeds = work.tile([P, HALVES, 2], F32, name="paths")
-        nc.vector.reduce_sum(
-            seeds[:],
-            eye[:].rearrange("p (h j) -> p j h", j=2).unsqueeze(1).to_broadcast([P, HALVES, 2, P // 2]),
-            axis=X_AXIS,
-        )
-        paths = seeds[:]
-        for s in range(1, LAST):
-            d = 1 << s
-            spread = held.tile([P, P], F32, name=f"spread{s}")
-            nc.vector.tensor_copy(
-                spread[:].rearrange("k (h b e) -> k h b e", b=2, e=d),
-                eye[:].rearrange("k (b h) -> k h b", b=2)[:, 0 : 64 // d, :].unsqueeze(3).to_broadcast([P, 64 // d, 2, d]),
-            )
-            steps = ring.tile([P, 2, HALVES, d], F32, name="steps")
-            nc.tensor.matmul(steps[:], spread[:], coef[:, :, 2 * d : 4 * d])
-            longer = work.tile([P, HALVES, 2, d], F32, name="paths")
-            nc.vector.tensor_tensor(
-                longer[:],
-                paths.unsqueeze(2).to_broadcast([P, HALVES, 2, d]),
-                steps[:].rearrange("p b t e -> p t b e"),
-                MULT,
-            )
-            paths = longer[:].rearrange("p t b e -> p t (b e)")
-
-        last = held.tile([P, 2, PICKED], F32, name="last")
-        for row in range(2):
-            nc.vector.tensor_tensor(
-                last[:, row, :].rearrange("p (g t e) -> p g t e", t=2, e=P),
-                paths.unsqueeze(1),
-                factors(trig, row, LAST),
-                MULT,
-            )
-
-        first_factors = held.tile([P, 2, PICKED], F32, name="first_factors")
-        for row in range(2):
-            nc.gpsimd.tensor_copy(
-                first_factors[:, row, :].rearrange("p (g t e) -> p g t e", t=2, e=1), factors(trig, row, 0)
-            )
+        flipped_blocks = []
         for b in range(BLOCKS):
             products = work.tile([P, 2, PICKED], F32, name="products")
-            for row in range(2):
+            for new_bit in range(2):
                 nc.vector.tensor_tensor(
-                    products[:, row, :], windows[b][:].indirect(offsets[:]), first_factors[:, row, :], MULT
+                    products[:, new_bit, :],
+                    windows[b][:].indirect(offsets[:]),
+                    first_factors[:, new_bit, :],
+                    MULT,
                 )
-            sides = products[:].rearrange("p r (g t) -> p g r t", t=2)
-            rotated = work.tile([P, PICKED], F32, name="rotated")
-            nc.vector.tensor_tensor(
-                rotated[:].rearrange("p (g r) -> p g r", r=2), sides[:, :, :, 0], sides[:, :, :, 1], ADD
-            )
-
-            flipped_psum = psum.tile([P, HALVES, P], F32, name=f"flipped_psum{b}")
-            for half in range(HALVES):
-                nc.tensor.transpose(flipped_psum[:, half, :], rotated[:, half * P : (half + 1) * P], eye[:])
-            flipped = work.tile([P, HALVES, P], F32, name="flipped")
+            sides = products[:].rearrange("p r (g t) -> p r t g", t=2)
+            flipped_psum = psum.tile([P, 2, P], F32, name=f"flipped_psum{b}")
+            for parity in range(2):
+                for side in range(2):
+                    nc.tensor.matmul(
+                        flipped_psum[:, parity, :],
+                        sides[:, parity, side, :],
+                        eye[:],
+                        is_transpose=True,
+                        start=(side == 0),
+                        stop=(side == 1),
+                    )
+            flipped = work.tile([P, 2, P], F32, name="flipped")
             nc.scalar.copy(flipped[:], flipped_psum[:])
+            flipped_blocks.append(flipped)
 
-            out_psum = psum.tile([P, PICKED], F32, name=f"out_psum{b}")
-            for half in range(HALVES):
+        halves = "p b (c e) -> p b c e"
+        paths = coef[:, :, 2:4]
+        for s in range(2, STAGES):
+            d = 1 << s
+            longer = held.tile([P, 2, d], F32, name=f"paths{s}")
+            nc.vector.tensor_tensor(
+                longer[:].rearrange(halves, c=2),
+                paths.unsqueeze(1).to_broadcast([P, 2, 2, d // 2]),
+                coef[:, :, d : 2 * d].rearrange(halves, c=2),
+                MULT,
+            )
+            paths = longer[:]
+        by_parity = paths.rearrange("p b (e r) -> p r b e", r=2)
+
+        for b in range(BLOCKS):
+            out_psum = psum.tile([P, 2, PAIRS], F32, name=f"out_psum{b}")
+            for parity in range(2):
                 nc.tensor.matmul(
-                    out_psum[:],
-                    flipped[:, half, :],
-                    last[:].rearrange("p r (t e) -> p t r e", t=HALVES)[:, half, :, :],
-                    start=(half == 0),
-                    stop=(half == HALVES - 1),
+                    out_psum[:, parity, :].rearrange("p (b e) -> p b e", b=2),
+                    flipped_blocks[b][:, parity, :],
+                    by_parity[:, parity, :, :],
                 )
-            result = work.tile([P, PICKED], F32, name="result")
-            nc.scalar.activation(result[:], out_psum[:], RELU)
-            nc.sync.dma_start(out[b * P : (b + 1) * P, :], result[:])
+            result = work.tile([P, PAIRS, 2], F32, name="result")
+            in_order = out_psum[:].rearrange("p r g -> p g r")
+            if b == 0:
+                nc.scalar.activation(result[:], in_order, RELU)
+            else:
+                nc.vector.tensor_scalar_max(result[:], in_order, 0.0)
+            nc.sync.dma_start(out[b * P : (b + 1) * P, :], result[:].rearrange("p g r -> p (g r)"))

@@ -29,8 +29,15 @@ def tile_quantumautoencoder_kernel(tc, x, theta, offs, out):
         tc.tile_pool(name="work", bufs=BLOCKS) as work,
         tc.psum_pool(name="psum", bufs=1) as psum,
     ):
-        first_angles = held.tile([P, ANGLES], F32, name="first_angles")
-        nc.sync.dma_start(first_angles[:], theta[:, 0:ANGLES].to_broadcast([P, ANGLES]))
+        table = held.tile([P, 2 * P], F32, name="table")
+        nc.vector.memset(table[:], 0.0)
+        by_stage = theta[0, :].rearrange("(s a) -> s a", a=ANGLES)
+        nc.sync.dma_start(table[0:2, P : 2 * P], by_stage[0 :: STAGES - 1, :])
+        for s in range(1, STAGES - 1):
+            d = 1 << s
+            runs = P // d
+            queue = nc.scalar if s <= 4 else nc.gpsimd
+            queue.dma_start(table[runs : 2 * runs, d : 2 * d], by_stage[s, :].rearrange("(h e) -> h e", e=d))
         offsets = held.tile([P, PICKED // 16], U16, name="offsets")
         nc.sync.dma_start(offsets[:], offs)
         windows = []
@@ -39,18 +46,10 @@ def tile_quantumautoencoder_kernel(tc, x, theta, offs, out):
             nc.sync.dma_start(window[:], x[b * P : (b + 1) * P, :])
             windows.append(window)
 
-        table = held.tile([P, 2 * P], F32, name="table")
-        nc.gpsimd.memset(table[:], 0.0)
-        for s in range(1, STAGES):
-            d = 1 << s
-            runs = P // d
-            nc.scalar.dma_start(
-                table[runs : 2 * runs, d : 2 * d],
-                theta[0, s * ANGLES : (s + 1) * ANGLES].rearrange("(h e) -> h e", e=d),
-            )
-
         quarter_turn = held.tile([P, 1], F32, name="quarter_turn")
         nc.vector.memset(quarter_turn[:], QUARTER_TURN)
+        warm = held.tile([P, 1], F32, name="warm")
+        nc.scalar.activation(warm[:], quarter_turn[:], SIN)
 
         first_phase = held.tile([P, PAIRS, 2], F32, name="first_phase")
         nc.vector.memset(first_phase[:, :, 0], 0.0)
@@ -67,17 +66,24 @@ def tile_quantumautoencoder_kernel(tc, x, theta, offs, out):
         phase = held.tile([P, 2 * P], F32, name="phase")
         nc.vector.tensor_scalar(phase[:, 2:], bits[:, 2:], QUARTER_TURN, None, MULT)
 
-        first_turns = held.tile([P, PAIRS, 2], F32, name="first_turns")
-        nc.vector.tensor_tensor(
-            first_turns[:], first_angles[:].unsqueeze(2).to_broadcast([P, PAIRS, 2]), first_phase[:], ADD
+        eye = held.tile([P, P], F32, name="eye")
+        make_identity(nc, eye[:])
+
+        from_row_0 = eye[:, 0:1].to_broadcast([P, P])
+        first_turns = psum.tile([P, PAIRS, 2], F32, name="first_turns")
+        nc.tensor.matmul(first_turns[:], from_row_0, first_phase[:], start=True, stop=False)
+        nc.tensor.matmul(
+            first_turns[:],
+            from_row_0,
+            table[:, P : 2 * P].unsqueeze(2).to_broadcast([P, PAIRS, 2]),
+            start=False,
+            stop=True,
         )
         first_factors = held.tile([P, 2, PICKED], F32, name="first_factors")
         flat_first_turns = first_turns[:].rearrange("p g t -> p (g t)")
         nc.scalar.activation(first_factors[:, 0, :], flat_first_turns, SIN, bias=quarter_turn[:], scale=-1.0)
         nc.scalar.activation(first_factors[:, 1, :], flat_first_turns, SIN)
 
-        eye = held.tile([P, P], F32, name="eye")
-        make_identity(nc, eye[:])
         spread = held.tile([P, P], F32, name="spread")
         for s in range(1, STAGES):
             d = 1 << s
@@ -85,9 +91,9 @@ def tile_quantumautoencoder_kernel(tc, x, theta, offs, out):
             takers = spread[:].rearrange("k (h e) -> k h e", e=d)
             own_run = eye[:, runs : 2 * runs].unsqueeze(2).to_broadcast([P, runs, d])
             if s == 1:
-                nc.gpsimd.tensor_copy(takers, own_run)
+                nc.vector.tensor_copy(takers, own_run)
             else:
-                nc.gpsimd.tensor_tensor(takers, takers, own_run, ADD)
+                nc.vector.tensor_tensor(takers, takers, own_run, ADD)
 
         turns = psum.tile([P, 2 * P], F32, name="turns")
         nc.tensor.matmul(turns[:, 2:], eye[:], phase[:, 2:], start=True, stop=False)

@@ -18,6 +18,7 @@ SAMPLES, UNITS, PICKED, ANGLES, STAGES = 256, 1024, 256, 128, 8
 BLOCKS = SAMPLES // P
 PAIRS = PICKED // 2
 QUARTER_TURN = math.pi / 2
+LATE_STAGES = 2
 
 FLOPS = SAMPLES * STAGES * ANGLES * 6
 
@@ -29,15 +30,21 @@ def tile_quantumautoencoder_kernel(tc, x, theta, offs, out):
         tc.tile_pool(name="work", bufs=BLOCKS) as work,
         tc.psum_pool(name="psum", bufs=1) as psum,
     ):
+        eye = held.tile([P, P], F32, name="eye")
+        make_identity(nc, eye[:])
+        row_number = held.tile([P, 1], I32, name="row_number")
+        nc.gpsimd.iota(row_number[:], pattern=[[0, 1]], base=0, channel_multiplier=1)
+
         table = held.tile([P, 2 * P], F32, name="table")
         nc.vector.memset(table[:], 0.0)
         by_stage = theta[0, :].rearrange("(s a) -> s a", a=ANGLES)
-        nc.sync.dma_start(table[0:2, P : 2 * P], by_stage[0 :: STAGES - 1, :])
-        for s in range(1, STAGES - 1):
+
+        def load_runs(queue, s):
             d = 1 << s
             runs = P // d
-            queue = nc.scalar if s <= 4 else nc.gpsimd
             queue.dma_start(table[runs : 2 * runs, d : 2 * d], by_stage[s, :].rearrange("(h e) -> h e", e=d))
+
+        nc.sync.dma_start(table[0:2, P : 2 * P], by_stage[0 :: STAGES - 1, :])
         offsets = held.tile([P, PICKED // 16], U16, name="offsets")
         nc.sync.dma_start(offsets[:], offs)
         windows = []
@@ -45,6 +52,10 @@ def tile_quantumautoencoder_kernel(tc, x, theta, offs, out):
             window = held.tile([P, UNITS], F32, name=f"window{b}")
             nc.sync.dma_start(window[:], x[b * P : (b + 1) * P, :])
             windows.append(window)
+        for s in range(STAGES - 2, LATE_STAGES, -1):
+            load_runs(nc.scalar, s)
+        for s in range(LATE_STAGES, 0, -1):
+            load_runs(nc.sync, s)
 
         quarter_turn = held.tile([P, 1], F32, name="quarter_turn")
         nc.vector.memset(quarter_turn[:], QUARTER_TURN)
@@ -55,8 +66,6 @@ def tile_quantumautoencoder_kernel(tc, x, theta, offs, out):
         nc.vector.memset(first_phase[:, :, 0], 0.0)
         nc.vector.memset(first_phase[:, :, 1], QUARTER_TURN)
 
-        row_number = held.tile([P, 1], I32, name="row_number")
-        nc.gpsimd.iota(row_number[:], pattern=[[0, 1]], base=0, channel_multiplier=1)
         bits = held.tile([P, 2 * P], I32, name="bits")
         for s in range(1, STAGES):
             d = 1 << s
@@ -65,9 +74,6 @@ def tile_quantumautoencoder_kernel(tc, x, theta, offs, out):
             )
         phase = held.tile([P, 2 * P], F32, name="phase")
         nc.vector.tensor_scalar(phase[:, 2:], bits[:, 2:], QUARTER_TURN, None, MULT)
-
-        eye = held.tile([P, P], F32, name="eye")
-        make_identity(nc, eye[:])
 
         from_row_0 = eye[:, 0:1].to_broadcast([P, P])
         first_turns = psum.tile([P, PAIRS, 2], F32, name="first_turns")
@@ -95,12 +101,14 @@ def tile_quantumautoencoder_kernel(tc, x, theta, offs, out):
             else:
                 nc.vector.tensor_tensor(takers, takers, own_run, ADD)
 
-        turns = psum.tile([P, 2 * P], F32, name="turns")
-        nc.tensor.matmul(turns[:, 2:], eye[:], phase[:, 2:], start=True, stop=False)
-        nc.tensor.matmul(turns[:, 2:], spread[:], table[:, 2:], start=False, stop=True)
         coef = held.tile([P, 2, 2 * P], F32, name="coef")
-        nc.scalar.activation(coef[:, 1, 2:], turns[:, 2:], SIN)
-        nc.scalar.activation(coef[:, 0, 2:], turns[:, 2:], SIN, bias=quarter_turn[:], scale=-1.0)
+        first_early = 2 << LATE_STAGES
+        for name, columns in (("turns", slice(first_early, 2 * P)), ("late_turns", slice(2, first_early))):
+            turns = psum.tile([P, columns.stop - columns.start], F32, name=name)
+            nc.tensor.matmul(turns[:], eye[:], phase[:, columns], start=True, stop=False)
+            nc.tensor.matmul(turns[:], spread[:], table[:, columns], start=False, stop=True)
+            nc.scalar.activation(coef[:, 1, columns], turns[:], SIN)
+            nc.scalar.activation(coef[:, 0, columns], turns[:], SIN, bias=quarter_turn[:], scale=-1.0)
 
         flipped_blocks = []
         for b in range(BLOCKS):
@@ -128,28 +136,35 @@ def tile_quantumautoencoder_kernel(tc, x, theta, offs, out):
             nc.scalar.copy(flipped[:], flipped_psum[:])
             flipped_blocks.append(flipped)
 
-        halves = "p b (c e) -> p b c e"
-        paths = coef[:, :, 2:4]
-        for s in range(2, STAGES):
+        def stage_pair(s):
             d = 1 << s
-            longer = held.tile([P, 2, d], F32, name=f"paths{s}")
+            pair = held.tile([P, 2, 2, d], F32, name=f"pair{s}")
             nc.vector.tensor_tensor(
-                longer[:].rearrange(halves, c=2),
-                paths.unsqueeze(1).to_broadcast([P, 2, 2, d // 2]),
-                coef[:, :, d : 2 * d].rearrange(halves, c=2),
+                pair[:],
+                coef[:, :, 2 * d : 4 * d].rearrange("p b (c e) -> p b c e", c=2),
+                coef[:, :, d : 2 * d].unsqueeze(1).to_broadcast([P, 2, 2, d]),
                 MULT,
             )
-            paths = longer[:]
-        by_parity = paths.rearrange("p b (e r) -> p r b e", r=2)
+            return pair[:].rearrange("p b c e -> p (b c e)")
+
+        def join(name, upper, lower):
+            repeats, period = upper.shape[1], upper.shape[2]
+            joined = held.tile([P, repeats, period], F32, name=name)
+            nc.vector.tensor_tensor(joined[:], upper, lower.unsqueeze(1).to_broadcast([P, repeats, period]), MULT)
+            return joined[:].rearrange("p a e -> p (a e)")
+
+        stages_5_6 = stage_pair(5)
+        stages_3_4 = stage_pair(3)
+        stages_5_7 = join("stages_5_7", coef[:, :, P : 2 * P], stages_5_6)
+        stages_1_2 = stage_pair(1)
+        stages_1_4 = join("stages_1_4", stages_3_4.rearrange("p (a e) -> p a e", e=8), stages_1_2)
+        matrix = join("matrix", stages_5_7.rearrange("p (a e) -> p a e", e=32), stages_1_4)
+        by_parity = matrix.rearrange("p (e r) -> p r e", r=2)
 
         for b in range(BLOCKS):
             out_psum = psum.tile([P, 2, PAIRS], F32, name=f"out_psum{b}")
             for parity in range(2):
-                nc.tensor.matmul(
-                    out_psum[:, parity, :].rearrange("p (b e) -> p b e", b=2),
-                    flipped_blocks[b][:, parity, :],
-                    by_parity[:, parity, :, :],
-                )
+                nc.tensor.matmul(out_psum[:, parity, :], flipped_blocks[b][:, parity, :], by_parity[:, parity, :])
             result = work.tile([P, PAIRS, 2], F32, name="result")
             in_order = out_psum[:].rearrange("p r g -> p g r")
             if b == 0:

@@ -128,7 +128,6 @@ def tile_quantumautoencoder_kernel(tc, x, theta, offs, out):
                         flipped_psum[:, parity, :],
                         sides[:, parity, side, :],
                         eye[:],
-                        is_transpose=True,
                         start=(side == 0),
                         stop=(side == 1),
                     )

@@ -35,16 +35,8 @@ def tile_quantumautoencoder_kernel(tc, x, theta, offs, out):
         row_number = held.tile([P, 1], I32, name="row_number")
         nc.gpsimd.iota(row_number[:], pattern=[[0, 1]], base=0, channel_multiplier=1)
 
-        table = held.tile([P, 2 * P], F32, name="table")
-        nc.vector.memset(table[:], 0.0)
-        by_stage = theta[0, :].rearrange("(s a) -> s a", a=ANGLES)
-
-        def load_runs(queue, s):
-            d = 1 << s
-            runs = P // d
-            queue.dma_start(table[runs : 2 * runs, d : 2 * d], by_stage[s, :].rearrange("(h e) -> h e", e=d))
-
-        nc.sync.dma_start(table[0:2, P : 2 * P], by_stage[0 :: STAGES - 1, :])
+        ends = held.tile([P, 2], F32, name="ends")
+        nc.sync.dma_start(ends[:], theta[0, :].rearrange("(s a) -> a s", a=ANGLES)[:, 0 :: STAGES - 1])
         offsets = held.tile([P, PICKED // 16], U16, name="offsets")
         nc.sync.dma_start(offsets[:], offs)
         windows = []
@@ -52,6 +44,18 @@ def tile_quantumautoencoder_kernel(tc, x, theta, offs, out):
             window = held.tile([P, UNITS], F32, name=f"window{b}")
             nc.sync.dma_start(window[:], x[b * P : (b + 1) * P, :])
             windows.append(window)
+
+        table = held.tile([P, P], F32, name="table")
+        nc.vector.memset(table[:], 0.0)
+
+        def load_runs(queue, s):
+            d = 1 << s
+            runs = P // d
+            queue.dma_start(
+                table[runs : 2 * runs, d : 2 * d],
+                theta[0, s * ANGLES : (s + 1) * ANGLES].rearrange("(h e) -> h e", e=d),
+            )
+
         for s in range(STAGES - 2, LATE_STAGES, -1):
             load_runs(nc.scalar, s)
         for s in range(LATE_STAGES, 0, -1):
@@ -62,36 +66,39 @@ def tile_quantumautoencoder_kernel(tc, x, theta, offs, out):
         warm = held.tile([P, 1], F32, name="warm")
         nc.scalar.activation(warm[:], quarter_turn[:], SIN)
 
-        first_phase = held.tile([P, PAIRS, 2], F32, name="first_phase")
-        nc.vector.memset(first_phase[:, :, 0], 0.0)
-        nc.vector.memset(first_phase[:, :, 1], QUARTER_TURN)
+        def spread_column(everywhere, column, start):
+            nc.tensor.matmul(everywhere, column.to_broadcast([P, P]), eye[:], is_transpose=True, start=start, stop=True)
 
-        bits = held.tile([P, 2 * P], I32, name="bits")
-        for s in range(1, STAGES):
+        first_turns = psum.tile([P, 2, PAIRS], F32, name="first_turns")
+        nc.tensor.matmul(first_turns[:, 1, :], eye[:], quarter_turn[:].to_broadcast([P, PAIRS]), start=True, stop=False)
+        spread_column(first_turns[:, 1, :], ends[:, 0:1], start=False)
+        spread_column(first_turns[:, 0, :], ends[:, 0:1], start=True)
+        first_factors = held.tile([P, 2, PAIRS, 2], F32, name="first_factors")
+        in_order = first_turns[:].rearrange("p t g -> p g t")
+        nc.scalar.activation(first_factors[:, 0, :, :], in_order, SIN, bias=quarter_turn[:], scale=-1.0)
+        nc.scalar.activation(first_factors[:, 1, :, :], in_order, SIN)
+
+        coef = held.tile([P, 2, 2 * P], F32, name="coef")
+        last_phase = held.tile([P, 2], F32, name="last_phase")
+        nc.vector.memset(last_phase[:], 0.0)
+        nc.vector.memset(last_phase[0 : P // 2, 0:1], QUARTER_TURN)
+        nc.vector.memset(last_phase[P // 2 : P, 1:2], QUARTER_TURN)
+        last_angles = psum.tile([P, ANGLES], F32, name="last_angles")
+        spread_column(last_angles[:], ends[:, 1:2], start=True)
+        nc.scalar.activation(coef[:, 1, P : 2 * P], last_angles[:], SIN, bias=last_phase[:, 1:2])
+        nc.scalar.activation(coef[:, 0, P : 2 * P], last_angles[:], SIN, bias=last_phase[:, 0:1], scale=-1.0)
+
+        bits = held.tile([P, P], I32, name="bits")
+        for s in range(1, STAGES - 1):
             d = 1 << s
             nc.vector.tensor_scalar(
                 bits[:, d : 2 * d], row_number[:].to_broadcast([P, d]), s - 1, 1, SHIFT_RIGHT, AND
             )
-        phase = held.tile([P, 2 * P], F32, name="phase")
+        phase = held.tile([P, P], F32, name="phase")
         nc.vector.tensor_scalar(phase[:, 2:], bits[:, 2:], QUARTER_TURN, None, MULT)
 
-        from_row_0 = eye[:, 0:1].to_broadcast([P, P])
-        first_turns = psum.tile([P, PAIRS, 2], F32, name="first_turns")
-        nc.tensor.matmul(first_turns[:], from_row_0, first_phase[:], start=True, stop=False)
-        nc.tensor.matmul(
-            first_turns[:],
-            from_row_0,
-            table[:, P : 2 * P].unsqueeze(2).to_broadcast([P, PAIRS, 2]),
-            start=False,
-            stop=True,
-        )
-        first_factors = held.tile([P, 2, PICKED], F32, name="first_factors")
-        flat_first_turns = first_turns[:].rearrange("p g t -> p (g t)")
-        nc.scalar.activation(first_factors[:, 0, :], flat_first_turns, SIN, bias=quarter_turn[:], scale=-1.0)
-        nc.scalar.activation(first_factors[:, 1, :], flat_first_turns, SIN)
-
         spread = held.tile([P, P], F32, name="spread")
-        for s in range(1, STAGES):
+        for s in range(1, STAGES - 1):
             d = 1 << s
             runs = P // d
             takers = spread[:].rearrange("k (h e) -> k h e", e=d)
@@ -101,23 +108,20 @@ def tile_quantumautoencoder_kernel(tc, x, theta, offs, out):
             else:
                 nc.vector.tensor_tensor(takers, takers, own_run, ADD)
 
-        coef = held.tile([P, 2, 2 * P], F32, name="coef")
-        first_early = 2 << LATE_STAGES
-        for name, columns in (("turns", slice(first_early, 2 * P)), ("late_turns", slice(2, first_early))):
+        def coefficients(name, columns):
             turns = psum.tile([P, columns.stop - columns.start], F32, name=name)
             nc.tensor.matmul(turns[:], eye[:], phase[:, columns], start=True, stop=False)
             nc.tensor.matmul(turns[:], spread[:], table[:, columns], start=False, stop=True)
             nc.scalar.activation(coef[:, 1, columns], turns[:], SIN)
             nc.scalar.activation(coef[:, 0, columns], turns[:], SIN, bias=quarter_turn[:], scale=-1.0)
 
-        flipped_blocks = []
-        for b in range(BLOCKS):
+        def first_stage(b):
             products = work.tile([P, 2, PICKED], F32, name="products")
             for new_bit in range(2):
                 nc.vector.tensor_tensor(
                     products[:, new_bit, :],
                     windows[b][:].indirect(offsets[:]),
-                    first_factors[:, new_bit, :],
+                    first_factors[:, new_bit, :, :].rearrange("p g t -> p (g t)"),
                     MULT,
                 )
             sides = products[:].rearrange("p r (g t) -> p r t g", t=2)
@@ -133,7 +137,13 @@ def tile_quantumautoencoder_kernel(tc, x, theta, offs, out):
                     )
             flipped = work.tile([P, 2, P], F32, name="flipped")
             nc.scalar.copy(flipped[:], flipped_psum[:])
-            flipped_blocks.append(flipped)
+            return flipped
+
+        first_early = 2 << LATE_STAGES
+        coefficients("turns", slice(first_early, P))
+        flipped_blocks = [first_stage(0)]
+        coefficients("late_turns", slice(2, first_early))
+        flipped_blocks.append(first_stage(1))
 
         def stage_pair(s):
             d = 1 << s

@@ -7,7 +7,6 @@ F32 = mybir.dt.float32
 I32 = mybir.dt.int32
 U16 = mybir.dt.uint16
 MULT = mybir.AluOpType.mult
-ADD = mybir.AluOpType.add
 SHIFT_RIGHT = mybir.AluOpType.logical_shift_right
 AND = mybir.AluOpType.bitwise_and
 SIN = mybir.ActivationFunctionType.Sin
@@ -101,12 +100,10 @@ def tile_quantumautoencoder_kernel(tc, x, theta, offs, out):
         for s in range(1, STAGES - 1):
             d = 1 << s
             runs = P // d
-            takers = spread[:].rearrange("k (h e) -> k h e", e=d)
-            own_run = eye[:, runs : 2 * runs].unsqueeze(2).to_broadcast([P, runs, d])
-            if s == 1:
-                nc.vector.tensor_copy(takers, own_run)
-            else:
-                nc.vector.tensor_tensor(takers, takers, own_run, ADD)
+            nc.vector.tensor_copy(
+                spread[0 : 2 * runs, :].rearrange("k (h e) -> k h e", e=d),
+                eye[0 : 2 * runs, runs : 2 * runs].unsqueeze(2).to_broadcast([2 * runs, runs, d]),
+            )
 
         def coefficients(name, columns):
             turns = psum.tile([P, columns.stop - columns.start], F32, name=name)

@@ -129,6 +129,7 @@ def tile_quantumautoencoder_kernel(tc, x, theta, offs, out):
                         flipped_psum[:, parity, :],
                         sides[:, parity, side, :],
                         eye[:],
+                        is_transpose=(b > 0),
                         start=(side == 0),
                         stop=(side == 1),
                     )
@@ -164,13 +165,19 @@ def tile_quantumautoencoder_kernel(tc, x, theta, offs, out):
         stages_5_7 = join("stages_5_7", coef[:, :, P : 2 * P], stages_5_6)
         stages_1_2 = stage_pair(1)
         stages_1_4 = join("stages_1_4", stages_3_4.rearrange("p (a e) -> p a e", e=8), stages_1_2)
-        matrix = join("matrix", stages_5_7.rearrange("p (a e) -> p a e", e=32), stages_1_4)
-        by_parity = matrix.rearrange("p (e r) -> p r e", r=2)
+        by_parity = [
+            join(
+                f"matrix{parity}",
+                stages_5_7.rearrange("p (a e r) -> p r a e", e=16, r=2)[:, parity, :, :],
+                stages_1_4.rearrange("p (e r) -> p r e", r=2)[:, parity, :],
+            )
+            for parity in range(2)
+        ]
 
         for b in range(BLOCKS):
             out_psum = psum.tile([P, 2, PAIRS], F32, name=f"out_psum{b}")
             for parity in range(2):
-                nc.tensor.matmul(out_psum[:, parity, :], flipped_blocks[b][:, parity, :], by_parity[:, parity, :])
+                nc.tensor.matmul(out_psum[:, parity, :], flipped_blocks[b][:, parity, :], by_parity[parity])
             result = work.tile([P, PAIRS, 2], F32, name="result")
             in_order = out_psum[:].rearrange("p r g -> p g r")
             if b == 0:

@@ -129,7 +129,7 @@ def tile_quantumautoencoder_kernel(tc, x, theta, offs, out):
                         flipped_psum[:, parity, :],
                         sides[:, parity, side, :],
                         eye[:],
-                        is_transpose=(b > 0),
+                        is_transpose=(b == 0),
                         start=(side == 0),
                         stop=(side == 1),
                     )

@@ -7,8 +7,14 @@ F32 = mybir.dt.float32
 I32 = mybir.dt.int32
 U16 = mybir.dt.uint16
 MULT = mybir.AluOpType.mult
+ADD = mybir.AluOpType.add
+SHIFT_LEFT = mybir.AluOpType.logical_shift_left
 SHIFT_RIGHT = mybir.AluOpType.logical_shift_right
 AND = mybir.AluOpType.bitwise_and
+XOR = mybir.AluOpType.bitwise_xor
+IS_LT = mybir.AluOpType.is_lt
+IS_EQUAL = mybir.AluOpType.is_equal
+FREE = mybir.AxisListType.X
 SIN = mybir.ActivationFunctionType.Sin
 RELU = mybir.ActivationFunctionType.Relu
 
@@ -17,7 +23,9 @@ SAMPLES, UNITS, PICKED, ANGLES, STAGES = 256, 1024, 256, 128, 8
 BLOCKS = SAMPLES // P
 PAIRS = PICKED // 2
 QUARTER_TURN = math.pi / 2
-LATE_STAGES = 2
+SHORT_STAGES, LONG_STAGES = range(1, 3), range(3, 7)
+SHORT, LONG = 2, 8
+PHASED = 32
 
 FLOPS = SAMPLES * STAGES * ANGLES * 6
 
@@ -29,10 +37,12 @@ def tile_quantumautoencoder_kernel(tc, x, theta, offs, out):
         tc.tile_pool(name="work", bufs=BLOCKS) as work,
         tc.psum_pool(name="psum", bufs=1) as psum,
     ):
+        row = held.tile([P, 1], I32, name="row")
+        nc.gpsimd.iota(row[:], pattern=[[0, 1]], base=0, channel_multiplier=1)
+        column = held.tile([P, P], I32, name="column")
+        nc.gpsimd.iota(column[:], pattern=[[1, P]], base=0, channel_multiplier=0)
         eye = held.tile([P, P], F32, name="eye")
         make_identity(nc, eye[:])
-        row_number = held.tile([P, 1], I32, name="row_number")
-        nc.gpsimd.iota(row_number[:], pattern=[[0, 1]], base=0, channel_multiplier=1)
 
         ends = held.tile([P, 2], F32, name="ends")
         nc.sync.dma_start(ends[:], theta[0, :].rearrange("(s a) -> a s", a=ANGLES)[:, 0 :: STAGES - 1])
@@ -43,22 +53,10 @@ def tile_quantumautoencoder_kernel(tc, x, theta, offs, out):
             window = held.tile([P, UNITS], F32, name=f"window{b}")
             nc.sync.dma_start(window[:], x[b * P : (b + 1) * P, :])
             windows.append(window)
-
-        table = held.tile([P, P], F32, name="table")
-        nc.vector.memset(table[:], 0.0)
-
-        def load_runs(queue, s):
-            d = 1 << s
-            runs = P // d
-            queue.dma_start(
-                table[runs : 2 * runs, d : 2 * d],
-                theta[0, s * ANGLES : (s + 1) * ANGLES].rearrange("(h e) -> h e", e=d),
-            )
-
-        for s in range(STAGES - 2, LATE_STAGES, -1):
-            load_runs(nc.scalar, s)
-        for s in range(LATE_STAGES, 0, -1):
-            load_runs(nc.sync, s)
+        long_rows = held.tile([P, LONG], F32, name="long_rows")
+        nc.scalar.dma_start(long_rows[:], theta[0, :].rearrange("(k e) -> k e", e=LONG))
+        short_rows = held.tile([P, SHORT], F32, name="short_rows")
+        nc.scalar.dma_start(short_rows[:], theta[0, ANGLES : 3 * ANGLES].rearrange("(k e) -> k e", e=SHORT))
 
         quarter_turn = held.tile([P, 1], F32, name="quarter_turn")
         nc.vector.memset(quarter_turn[:], QUARTER_TURN)
@@ -87,30 +85,73 @@ def tile_quantumautoencoder_kernel(tc, x, theta, offs, out):
         nc.scalar.activation(coef[:, 1, P : 2 * P], last_angles[:], SIN, bias=last_phase[:, 1:2])
         nc.scalar.activation(coef[:, 0, P : 2 * P], last_angles[:], SIN, bias=last_phase[:, 0:1], scale=-1.0)
 
-        bits = held.tile([P, P], I32, name="bits")
-        for s in range(1, STAGES - 1):
-            d = 1 << s
-            nc.vector.tensor_scalar(
-                bits[:, d : 2 * d], row_number[:].to_broadcast([P, d]), s - 1, 1, SHIFT_RIGHT, AND
-            )
-        phase = held.tile([P, P], F32, name="phase")
-        nc.vector.tensor_scalar(phase[:, 2:], bits[:, 2:], QUARTER_TURN, None, MULT)
+        shifted = held.tile([PHASED, P], I32, name="shifted")
+        nc.vector.tensor_tensor(shifted[:], column[0:PHASED, :], row[0:PHASED, :].to_broadcast([PHASED, P]), SHIFT_RIGHT)
+        halved = held.tile([PHASED, P], I32, name="halved")
+        nc.vector.tensor_scalar(halved[:], shifted[:], 1, None, SHIFT_RIGHT)
+        bit_of = held.tile([PHASED, P], F32, name="bit_of")
+        nc.vector.scalar_tensor_tensor(bit_of[:], halved[:], -2.0, shifted[:], MULT, ADD)
+        at_stage = held.tile([PHASED, P], F32, name="at_stage")
+        nc.vector.tensor_scalar(at_stage[:], halved[:], 1, QUARTER_TURN, IS_EQUAL, MULT)
 
-        spread = held.tile([P, P], F32, name="spread")
-        for s in range(1, STAGES - 1):
-            d = 1 << s
-            runs = P // d
-            nc.vector.tensor_copy(
-                spread[0 : 2 * runs, :].rearrange("k (h e) -> k h e", e=d),
-                eye[0 : 2 * runs, runs : 2 * runs].unsqueeze(2).to_broadcast([2 * runs, runs, d]),
-            )
+        def spread_matrix(name, width, first):
+            base = held.tile([P, 1], I32, name=f"{name}_base")
+            nc.vector.tensor_scalar(base[:], row[:], width.bit_length() - 1, ANGLES - 1, SHIFT_LEFT, AND)
+            first_run = held.tile([P, 1], I32, name=f"{name}_first_run")
+            nc.vector.memset(first_run[:], 1 << first)
+            stage = held.tile([P, 1], I32, name=f"{name}_stage")
+            nc.vector.tensor_scalar(stage[:], row[:], (ANGLES // width).bit_length() - 1, None, SHIFT_RIGHT)
+            apart = held.tile([P, P], I32, name=f"{name}_apart")
+            nc.vector.tensor_tensor(apart[:], column[:], base[:].to_broadcast([P, P]), XOR)
+            run = held.tile([P, 1], I32, name=f"{name}_run")
+            nc.vector.tensor_tensor(run[:], first_run[:], stage[:], SHIFT_LEFT)
+            spread = held.tile([P, P], F32, name=f"{name}_spread")
+            nc.vector.tensor_tensor(spread[:], apart[:], run[:].to_broadcast([P, P]), IS_LT)
+            return spread
 
-        def coefficients(name, columns):
-            turns = psum.tile([P, columns.stop - columns.start], F32, name=name)
-            nc.tensor.matmul(turns[:], eye[:], phase[:, columns], start=True, stop=False)
-            nc.tensor.matmul(turns[:], spread[:], table[:, columns], start=False, stop=True)
-            nc.scalar.activation(coef[:, 1, columns], turns[:], SIN)
-            nc.scalar.activation(coef[:, 0, columns], turns[:], SIN, bias=quarter_turn[:], scale=-1.0)
+        def places(name, width, first, stages):
+            rows = ANGLES // width
+            place = held.tile([P, (1 << stages.stop) // width - 1], F32, name=f"{name}_place")
+            for s in stages:
+                parts = (1 << s) // width
+                stage_rows = eye[:, (s - first) * rows : (s - first + 1) * rows]
+                nc.vector.tensor_reduce(
+                    place[:, parts - 1 : 2 * parts - 1], stage_rows.rearrange("k (h q) -> k q h", q=parts), FREE, ADD
+                )
+            return place
+
+        def put_in_place(name, rows, place):
+            shape = [P, place.shape[1], rows.shape[1]]
+            placed = held.tile(shape, F32, name=name)
+            nc.vector.tensor_tensor(
+                placed[:], rows[:].unsqueeze(1).to_broadcast(shape), place[:].unsqueeze(2).to_broadcast(shape), MULT
+            )
+            return placed[:].rearrange("k c e -> k (c e)")
+
+        long_turns = psum.tile([P, P - LONG], F32, name="long_turns")
+        nc.tensor.matmul(long_turns[:], bit_of[:], at_stage[:, LONG:], start=True, stop=False)
+        long_spread, long_place = spread_matrix("long", LONG, 0), places("long", LONG, 0, LONG_STAGES)
+        short_spread, short_place = spread_matrix("short", SHORT, 1), places("short", SHORT, 1, SHORT_STAGES)
+        long_placed = put_in_place("long_placed", long_rows, long_place)
+        nc.tensor.matmul(long_turns[:], long_spread[:], long_placed, start=False, stop=True)
+        nc.scalar.activation(coef[:, 1, LONG:P], long_turns[:], SIN)
+        nc.scalar.activation(coef[:, 0, LONG:P], long_turns[:], SIN, bias=quarter_turn[:], scale=-1.0)
+
+        short_bits = held.tile([P, len(SHORT_STAGES)], I32, name="short_bits")
+        for i, s in enumerate(SHORT_STAGES):
+            nc.vector.tensor_scalar(short_bits[:, i : i + 1], row[:], s - 1, 1, SHIFT_RIGHT, AND)
+        short_phase = held.tile([P, len(SHORT_STAGES)], F32, name="short_phase")
+        nc.vector.tensor_scalar(short_phase[:], short_bits[:], QUARTER_TURN, None, MULT)
+        rest_of_turn = held.tile([P, len(SHORT_STAGES)], F32, name="rest_of_turn")
+        nc.vector.tensor_scalar(rest_of_turn[:], short_bits[:], -QUARTER_TURN, QUARTER_TURN, MULT, ADD)
+        short_placed = put_in_place("short_placed", short_rows, short_place)
+        short_turns = psum.tile([P, LONG - SHORT], F32, name="short_turns")
+        nc.tensor.matmul(short_turns[:], short_spread[:], short_placed, start=True, stop=True)
+        for i, s in enumerate(SHORT_STAGES):
+            columns = slice(1 << s, 2 << s)
+            angles = short_turns[:, columns.start - SHORT : columns.stop - SHORT]
+            nc.scalar.activation(coef[:, 1, columns], angles, SIN, bias=short_phase[:, i : i + 1])
+            nc.scalar.activation(coef[:, 0, columns], angles, SIN, bias=rest_of_turn[:, i : i + 1], scale=-1.0)
 
         def first_stage(b):
             products = work.tile([P, 2, PICKED], F32, name="products")
@@ -129,7 +170,7 @@ def tile_quantumautoencoder_kernel(tc, x, theta, offs, out):
                         flipped_psum[:, parity, :],
                         sides[:, parity, side, :],
                         eye[:],
-                        is_transpose=(b == 0),
+                        is_transpose=(b == BLOCKS - 1),
                         start=(side == 0),
                         stop=(side == 1),
                     )
@@ -137,11 +178,7 @@ def tile_quantumautoencoder_kernel(tc, x, theta, offs, out):
             nc.scalar.copy(flipped[:], flipped_psum[:])
             return flipped
 
-        first_early = 2 << LATE_STAGES
-        coefficients("turns", slice(first_early, P))
-        flipped_blocks = [first_stage(0)]
-        coefficients("late_turns", slice(2, first_early))
-        flipped_blocks.append(first_stage(1))
+        flipped_blocks = [first_stage(b) for b in range(BLOCKS)]
 
         def stage_pair(s):
             d = 1 << s
@@ -174,12 +211,13 @@ def tile_quantumautoencoder_kernel(tc, x, theta, offs, out):
             for parity in range(2)
         ]
 
+        out_psums = [psum.tile([P, 2, PAIRS], F32, name=f"out_psum{b}") for b in range(BLOCKS)]
+        for parity in range(2):
+            for b in range(BLOCKS):
+                nc.tensor.matmul(out_psums[b][:, parity, :], flipped_blocks[b][:, parity, :], by_parity[parity])
         for b in range(BLOCKS):
-            out_psum = psum.tile([P, 2, PAIRS], F32, name=f"out_psum{b}")
-            for parity in range(2):
-                nc.tensor.matmul(out_psum[:, parity, :], flipped_blocks[b][:, parity, :], by_parity[parity])
             result = work.tile([P, PAIRS, 2], F32, name="result")
-            in_order = out_psum[:].rearrange("p r g -> p g r")
+            in_order = out_psums[b][:].rearrange("p r g -> p g r")
             if b == 0:
                 nc.scalar.activation(result[:], in_order, RELU)
             else:

@@ -1,7 +1,6 @@
 import math
 
 import concourse.mybir as mybir
-from concourse.masks import make_identity
 
 F32 = mybir.dt.float32
 I32 = mybir.dt.int32
@@ -25,7 +24,6 @@ PAIRS = PICKED // 2
 QUARTER_TURN = math.pi / 2
 SHORT_STAGES, LONG_STAGES = range(1, 3), range(3, 7)
 SHORT, LONG = 2, 8
-PHASED = 32
 
 FLOPS = SAMPLES * STAGES * ANGLES * 6
 
@@ -42,7 +40,7 @@ def tile_quantumautoencoder_kernel(tc, x, theta, offs, out):
         column = held.tile([P, P], I32, name="column")
         nc.gpsimd.iota(column[:], pattern=[[1, P]], base=0, channel_multiplier=0)
         eye = held.tile([P, P], F32, name="eye")
-        make_identity(nc, eye[:])
+        nc.vector.tensor_tensor(eye[:], column[:], row[:].to_broadcast([P, P]), IS_EQUAL)
 
         ends = held.tile([P, 2], F32, name="ends")
         nc.sync.dma_start(ends[:], theta[0, :].rearrange("(s a) -> a s", a=ANGLES)[:, 0 :: STAGES - 1])
@@ -63,106 +61,99 @@ def tile_quantumautoencoder_kernel(tc, x, theta, offs, out):
         warm = held.tile([P, 1], F32, name="warm")
         nc.scalar.activation(warm[:], quarter_turn[:], SIN)
 
-        def spread_column(everywhere, column, start):
-            nc.tensor.matmul(everywhere, column.to_broadcast([P, P]), eye[:], is_transpose=True, start=start, stop=True)
+        def spread_column(everywhere, angles, start=True, stop=True):
+            nc.tensor.matmul(everywhere, angles.to_broadcast([P, P]), eye[:], is_transpose=True, start=start, stop=stop)
 
         first_turns = psum.tile([P, 2, PAIRS], F32, name="first_turns")
-        nc.tensor.matmul(first_turns[:, 1, :], eye[:], quarter_turn[:].to_broadcast([P, PAIRS]), start=True, stop=False)
+        spread_column(first_turns[:, 1, :], quarter_turn[:], stop=False)
         spread_column(first_turns[:, 1, :], ends[:, 0:1], start=False)
-        spread_column(first_turns[:, 0, :], ends[:, 0:1], start=True)
+        spread_column(first_turns[:, 0, :], ends[:, 0:1])
         first_factors = held.tile([P, 2, PAIRS, 2], F32, name="first_factors")
         in_order = first_turns[:].rearrange("p t g -> p g t")
         nc.scalar.activation(first_factors[:, 0, :, :], in_order, SIN, bias=quarter_turn[:], scale=-1.0)
         nc.scalar.activation(first_factors[:, 1, :, :], in_order, SIN)
 
         coef = held.tile([P, 2, 2 * P], F32, name="coef")
-        last_phase = held.tile([P, 2], F32, name="last_phase")
-        nc.vector.memset(last_phase[:], 0.0)
-        nc.vector.memset(last_phase[0 : P // 2, 0:1], QUARTER_TURN)
-        nc.vector.memset(last_phase[P // 2 : P, 1:2], QUARTER_TURN)
+        late = STAGES - 1
+        shifted = held.tile([P, late], I32, name="shifted")
+        nc.vector.tensor_tensor(shifted[:], row[:].to_broadcast([P, late]), column[:, :late], SHIFT_RIGHT)
+        bit = held.tile([P, late], I32, name="bit")
+        nc.vector.tensor_scalar(bit[:], shifted[:], 1, None, AND)
+        bias = held.tile([P, 2, late], F32, name="bias")
+        nc.vector.tensor_scalar(bias[:, 1, :], bit[:], QUARTER_TURN, None, MULT)
+        nc.vector.tensor_scalar(bias[:, 0, :], bit[:], -QUARTER_TURN, QUARTER_TURN, MULT, ADD)
+
+        def sines(s, angles):
+            columns = slice(1 << s, 2 << s)
+            nc.scalar.activation(coef[:, 1, columns], angles, SIN, bias=bias[:, 1, s - 1 : s])
+            nc.scalar.activation(coef[:, 0, columns], angles, SIN, bias=bias[:, 0, s - 1 : s], scale=-1.0)
+
         last_angles = psum.tile([P, ANGLES], F32, name="last_angles")
-        spread_column(last_angles[:], ends[:, 1:2], start=True)
-        nc.scalar.activation(coef[:, 1, P : 2 * P], last_angles[:], SIN, bias=last_phase[:, 1:2])
-        nc.scalar.activation(coef[:, 0, P : 2 * P], last_angles[:], SIN, bias=last_phase[:, 0:1], scale=-1.0)
+        spread_column(last_angles[:], ends[:, 1:2])
+        sines(late, last_angles[:])
 
-        shifted = held.tile([PHASED, P], I32, name="shifted")
-        nc.vector.tensor_tensor(shifted[:], column[0:PHASED, :], row[0:PHASED, :].to_broadcast([PHASED, P]), SHIFT_RIGHT)
-        halved = held.tile([PHASED, P], I32, name="halved")
-        nc.vector.tensor_scalar(halved[:], shifted[:], 1, None, SHIFT_RIGHT)
-        bit_of = held.tile([PHASED, P], F32, name="bit_of")
-        nc.vector.scalar_tensor_tensor(bit_of[:], halved[:], -2.0, shifted[:], MULT, ADD)
-        at_stage = held.tile([PHASED, P], F32, name="at_stage")
-        nc.vector.tensor_scalar(at_stage[:], halved[:], 1, QUARTER_TURN, IS_EQUAL, MULT)
+        base = held.tile([P, 1], I32, name="base")
+        nc.vector.tensor_scalar(base[:], row[:], 3, ANGLES - 1, SHIFT_LEFT, AND)
+        run = held.tile([P, 1], I32, name="run")
+        nc.vector.tensor_tensor(run[:], column[:, 1:2], shifted[:, 4:5], SHIFT_LEFT)
+        apart = held.tile([P, P], I32, name="apart")
+        nc.vector.tensor_tensor(apart[:], column[:], base[:].to_broadcast([P, P]), XOR)
 
-        def spread_matrix(name, width, first):
-            base = held.tile([P, 1], I32, name=f"{name}_base")
-            nc.vector.tensor_scalar(base[:], row[:], width.bit_length() - 1, ANGLES - 1, SHIFT_LEFT, AND)
-            first_run = held.tile([P, 1], I32, name=f"{name}_first_run")
-            nc.vector.memset(first_run[:], 1 << first)
-            stage = held.tile([P, 1], I32, name=f"{name}_stage")
-            nc.vector.tensor_scalar(stage[:], row[:], (ANGLES // width).bit_length() - 1, None, SHIFT_RIGHT)
-            apart = held.tile([P, P], I32, name=f"{name}_apart")
-            nc.vector.tensor_tensor(apart[:], column[:], base[:].to_broadcast([P, P]), XOR)
-            run = held.tile([P, 1], I32, name=f"{name}_run")
-            nc.vector.tensor_tensor(run[:], first_run[:], stage[:], SHIFT_LEFT)
-            spread = held.tile([P, P], F32, name=f"{name}_spread")
-            nc.vector.tensor_tensor(spread[:], apart[:], run[:].to_broadcast([P, P]), IS_LT)
-            return spread
+        long_place = held.tile([P, P // LONG - 1], F32, name="long_place")
+        for s in LONG_STAGES:
+            parts = (1 << s) // LONG
+            stage_rows = eye[:, s * ANGLES // LONG : (s + 1) * ANGLES // LONG]
+            nc.vector.tensor_reduce(
+                long_place[:, parts - 1 : 2 * parts - 1], stage_rows.rearrange("k (h q) -> k q h", q=parts), FREE, ADD
+            )
+        long_spread = held.tile([P, P], F32, name="long_spread")
+        nc.vector.tensor_tensor(long_spread[:], apart[:], run[:].to_broadcast([P, P]), IS_LT)
 
-        def places(name, width, first, stages):
-            rows = ANGLES // width
-            place = held.tile([P, (1 << stages.stop) // width - 1], F32, name=f"{name}_place")
-            for s in stages:
-                parts = (1 << s) // width
-                stage_rows = eye[:, (s - first) * rows : (s - first + 1) * rows]
-                nc.vector.tensor_reduce(
-                    place[:, parts - 1 : 2 * parts - 1], stage_rows.rearrange("k (h q) -> k q h", q=parts), FREE, ADD
-                )
-            return place
+        half = P // 2
+        short_spread = held.tile([P, P], F32, name="short_spread")
+        nc.vector.tensor_copy(
+            short_spread[:half, :].rearrange("k (h e) -> k h e", e=2),
+            eye[:half, :half].unsqueeze(2).to_broadcast([half, half, 2]),
+        )
+        nc.vector.tensor_tensor(
+            short_spread[half:, :].rearrange("k (h e) -> k h e", e=4),
+            eye[half:, half::2].unsqueeze(2).to_broadcast([half, half // 2, 4]),
+            eye[half:, half + 1 :: 2].unsqueeze(2).to_broadcast([half, half // 2, 4]),
+            ADD,
+        )
+        short_place = held.tile([P, 3], F32, name="short_place")
+        nc.vector.tensor_reduce(short_place[:, 0:1], eye[:, :half], FREE, ADD)
+        nc.vector.tensor_reduce(short_place[:, 1:3], eye[:, half:].rearrange("k (h q) -> k q h", q=2), FREE, ADD)
 
-        def put_in_place(name, rows, place):
+        def own_angles(name, rows, place, spread):
             shape = [P, place.shape[1], rows.shape[1]]
-            placed = held.tile(shape, F32, name=name)
+            placed = held.tile(shape, F32, name=f"{name}_placed")
             nc.vector.tensor_tensor(
                 placed[:], rows[:].unsqueeze(1).to_broadcast(shape), place[:].unsqueeze(2).to_broadcast(shape), MULT
             )
-            return placed[:].rearrange("k c e -> k (c e)")
+            angles = psum.tile([P, shape[1] * shape[2]], F32, name=f"{name}_angles")
+            nc.tensor.matmul(angles[:], spread[:], placed[:].rearrange("k c e -> k (c e)"), start=True, stop=True)
+            return angles
 
-        long_turns = psum.tile([P, P - LONG], F32, name="long_turns")
-        nc.tensor.matmul(long_turns[:], bit_of[:], at_stage[:, LONG:], start=True, stop=False)
-        long_spread, long_place = spread_matrix("long", LONG, 0), places("long", LONG, 0, LONG_STAGES)
-        short_spread, short_place = spread_matrix("short", SHORT, 1), places("short", SHORT, 1, SHORT_STAGES)
-        long_placed = put_in_place("long_placed", long_rows, long_place)
-        nc.tensor.matmul(long_turns[:], long_spread[:], long_placed, start=False, stop=True)
-        nc.scalar.activation(coef[:, 1, LONG:P], long_turns[:], SIN)
-        nc.scalar.activation(coef[:, 0, LONG:P], long_turns[:], SIN, bias=quarter_turn[:], scale=-1.0)
+        long_angles = own_angles("long", long_rows, long_place, long_spread)
+        for s in LONG_STAGES:
+            sines(s, long_angles[:, (1 << s) - LONG : (2 << s) - LONG])
+        short_angles = own_angles("short", short_rows, short_place, short_spread)
+        for s in SHORT_STAGES:
+            sines(s, short_angles[:, (1 << s) - SHORT : (2 << s) - SHORT])
 
-        short_bits = held.tile([P, len(SHORT_STAGES)], I32, name="short_bits")
-        for i, s in enumerate(SHORT_STAGES):
-            nc.vector.tensor_scalar(short_bits[:, i : i + 1], row[:], s - 1, 1, SHIFT_RIGHT, AND)
-        short_phase = held.tile([P, len(SHORT_STAGES)], F32, name="short_phase")
-        nc.vector.tensor_scalar(short_phase[:], short_bits[:], QUARTER_TURN, None, MULT)
-        rest_of_turn = held.tile([P, len(SHORT_STAGES)], F32, name="rest_of_turn")
-        nc.vector.tensor_scalar(rest_of_turn[:], short_bits[:], -QUARTER_TURN, QUARTER_TURN, MULT, ADD)
-        short_placed = put_in_place("short_placed", short_rows, short_place)
-        short_turns = psum.tile([P, LONG - SHORT], F32, name="short_turns")
-        nc.tensor.matmul(short_turns[:], short_spread[:], short_placed, start=True, stop=True)
-        for i, s in enumerate(SHORT_STAGES):
-            columns = slice(1 << s, 2 << s)
-            angles = short_turns[:, columns.start - SHORT : columns.stop - SHORT]
-            nc.scalar.activation(coef[:, 1, columns], angles, SIN, bias=short_phase[:, i : i + 1])
-            nc.scalar.activation(coef[:, 0, columns], angles, SIN, bias=rest_of_turn[:, i : i + 1], scale=-1.0)
+        products = [work.tile([P, 2, PICKED], F32, name="products") for b in range(BLOCKS)]
 
-        def first_stage(b):
-            products = work.tile([P, 2, PICKED], F32, name="products")
-            for new_bit in range(2):
-                nc.vector.tensor_tensor(
-                    products[:, new_bit, :],
-                    windows[b][:].indirect(offsets[:]),
-                    first_factors[:, new_bit, :, :].rearrange("p g t -> p (g t)"),
-                    MULT,
-                )
-            sides = products[:].rearrange("p r (g t) -> p r t g", t=2)
+        def rotate(b, new_bit):
+            nc.vector.tensor_tensor(
+                products[b][:, new_bit, :],
+                windows[b][:].indirect(offsets[:]),
+                first_factors[:, new_bit, :, :].rearrange("p g t -> p (g t)"),
+                MULT,
+            )
+
+        def flip(b):
+            sides = products[b][:].rearrange("p r (g t) -> p r t g", t=2)
             flipped_psum = psum.tile([P, 2, P], F32, name=f"flipped_psum{b}")
             for parity in range(2):
                 for side in range(2):
@@ -177,8 +168,6 @@ def tile_quantumautoencoder_kernel(tc, x, theta, offs, out):
             flipped = work.tile([P, 2, P], F32, name="flipped")
             nc.scalar.copy(flipped[:], flipped_psum[:])
             return flipped
-
-        flipped_blocks = [first_stage(b) for b in range(BLOCKS)]
 
         def stage_pair(s):
             d = 1 << s
@@ -197,16 +186,29 @@ def tile_quantumautoencoder_kernel(tc, x, theta, offs, out):
             nc.vector.tensor_tensor(joined[:], upper, lower.unsqueeze(1).to_broadcast([P, repeats, period]), MULT)
             return joined[:].rearrange("p a e -> p (a e)")
 
-        stages_5_6 = stage_pair(5)
-        stages_3_4 = stage_pair(3)
-        stages_5_7 = join("stages_5_7", coef[:, :, P : 2 * P], stages_5_6)
+        rotate(0, 0)
+        rotate(0, 1)
+        flipped_blocks = [flip(0)]
+        rotate(1, 0)
         stages_1_2 = stage_pair(1)
+        stages_3_4 = stage_pair(3)
+        stages_5_6 = stage_pair(5)
         stages_1_4 = join("stages_1_4", stages_3_4.rearrange("p (a e) -> p a e", e=8), stages_1_2)
+        rotate(1, 1)
+        flipped_blocks.append(flip(1))
+        stages_1_6 = [
+            join(
+                f"stages_1_6_{parity}",
+                stages_5_6.rearrange("p (a e r) -> p r a e", e=16, r=2)[:, parity, :, :],
+                stages_1_4.rearrange("p (e r) -> p r e", r=2)[:, parity, :],
+            )
+            for parity in range(2)
+        ]
         by_parity = [
             join(
                 f"matrix{parity}",
-                stages_5_7.rearrange("p (a e r) -> p r a e", e=16, r=2)[:, parity, :, :],
-                stages_1_4.rearrange("p (e r) -> p r e", r=2)[:, parity, :],
+                coef[:, :, P : 2 * P].rearrange("p b (e r) -> p r b e", r=2)[:, parity, :, :],
+                stages_1_6[parity],
             )
             for parity in range(2)
         ]

@@ -161,7 +161,7 @@ def tile_quantumautoencoder_kernel(tc, x, theta, offs, out):
                         flipped_psum[:, parity, :],
                         sides[:, parity, side, :],
                         eye[:],
-                        is_transpose=(b == BLOCKS - 1),
+                        is_transpose=not (b == 0 and parity == 1),
                         start=(side == 0),
                         stop=(side == 1),
                     )

import math

import concourse.mybir as mybir

F32 = mybir.dt.float32
I32 = mybir.dt.int32
U16 = mybir.dt.uint16
MULT = mybir.AluOpType.mult
ADD = mybir.AluOpType.add
SHIFT_LEFT = mybir.AluOpType.logical_shift_left
SHIFT_RIGHT = mybir.AluOpType.logical_shift_right
AND = mybir.AluOpType.bitwise_and
XOR = mybir.AluOpType.bitwise_xor
IS_LT = mybir.AluOpType.is_lt
IS_EQUAL = mybir.AluOpType.is_equal
FREE = mybir.AxisListType.X
SIN = mybir.ActivationFunctionType.Sin
RELU = mybir.ActivationFunctionType.Relu

P = 128
SAMPLES, UNITS, PICKED, ANGLES, STAGES = 256, 1024, 256, 128, 8
BLOCKS = SAMPLES // P
PAIRS = PICKED // 2
QUARTER_TURN = math.pi / 2
SHORT_STAGES, LONG_STAGES = range(1, 3), range(3, 7)
SHORT, LONG = 2, 8

FLOPS = SAMPLES * STAGES * ANGLES * 6


def tile_quantumautoencoder_kernel(tc, x, theta, offs, out):
    nc = tc.nc
    with (
        tc.tile_pool(name="held", bufs=1) as held,
        tc.tile_pool(name="work", bufs=BLOCKS) as work,
        tc.psum_pool(name="psum", bufs=1) as psum,
    ):
        row = held.tile([P, 1], I32, name="row")
        nc.gpsimd.iota(row[:], pattern=[[0, 1]], base=0, channel_multiplier=1)
        column = held.tile([P, P], I32, name="column")
        nc.gpsimd.iota(column[:], pattern=[[1, P]], base=0, channel_multiplier=0)
        eye = held.tile([P, P], F32, name="eye")
        nc.vector.tensor_tensor(eye[:], column[:], row[:].to_broadcast([P, P]), IS_EQUAL)

        ends = held.tile([P, 2], F32, name="ends")
        nc.sync.dma_start(ends[:], theta[0, :].rearrange("(s a) -> a s", a=ANGLES)[:, 0 :: STAGES - 1])
        offsets = held.tile([P, PICKED // 16], U16, name="offsets")
        nc.sync.dma_start(offsets[:], offs)
        windows = []
        for b in range(BLOCKS):
            window = held.tile([P, UNITS], F32, name=f"window{b}")
            nc.sync.dma_start(window[:], x[b * P : (b + 1) * P, :])
            windows.append(window)
        long_rows = held.tile([P, LONG], F32, name="long_rows")
        nc.scalar.dma_start(long_rows[:], theta[0, :].rearrange("(k e) -> k e", e=LONG))
        short_rows = held.tile([P, SHORT], F32, name="short_rows")
        nc.scalar.dma_start(short_rows[:], theta[0, ANGLES : 3 * ANGLES].rearrange("(k e) -> k e", e=SHORT))

        quarter_turn = held.tile([P, 1], F32, name="quarter_turn")
        nc.vector.memset(quarter_turn[:], QUARTER_TURN)
        warm = held.tile([P, 1], F32, name="warm")
        nc.scalar.activation(warm[:], quarter_turn[:], SIN)

        def spread_column(everywhere, angles, start=True, stop=True):
            nc.tensor.matmul(everywhere, angles.to_broadcast([P, P]), eye[:], is_transpose=True, start=start, stop=stop)

        first_turns = psum.tile([P, 2, PAIRS], F32, name="first_turns")
        spread_column(first_turns[:, 1, :], quarter_turn[:], stop=False)
        spread_column(first_turns[:, 1, :], ends[:, 0:1], start=False)
        spread_column(first_turns[:, 0, :], ends[:, 0:1])
        first_factors = held.tile([P, 2, PAIRS, 2], F32, name="first_factors")
        in_order = first_turns[:].rearrange("p t g -> p g t")
        nc.scalar.activation(first_factors[:, 0, :, :], in_order, SIN, bias=quarter_turn[:], scale=-1.0)
        nc.scalar.activation(first_factors[:, 1, :, :], in_order, SIN)

        coef = held.tile([P, 2, 2 * P], F32, name="coef")
        late = STAGES - 1
        shifted = held.tile([P, late], I32, name="shifted")
        nc.vector.tensor_tensor(shifted[:], row[:].to_broadcast([P, late]), column[:, :late], SHIFT_RIGHT)
        bit = held.tile([P, late], I32, name="bit")
        nc.vector.tensor_scalar(bit[:], shifted[:], 1, None, AND)
        bias = held.tile([P, 2, late], F32, name="bias")
        nc.vector.tensor_scalar(bias[:, 1, :], bit[:], QUARTER_TURN, None, MULT)
        nc.vector.tensor_scalar(bias[:, 0, :], bit[:], -QUARTER_TURN, QUARTER_TURN, MULT, ADD)

        def sines(s, angles):
            columns = slice(1 << s, 2 << s)
            nc.scalar.activation(coef[:, 1, columns], angles, SIN, bias=bias[:, 1, s - 1 : s])
            nc.scalar.activation(coef[:, 0, columns], angles, SIN, bias=bias[:, 0, s - 1 : s], scale=-1.0)

        last_angles = psum.tile([P, ANGLES], F32, name="last_angles")
        spread_column(last_angles[:], ends[:, 1:2])
        sines(late, last_angles[:])

        base = held.tile([P, 1], I32, name="base")
        nc.vector.tensor_scalar(base[:], row[:], 3, ANGLES - 1, SHIFT_LEFT, AND)
        run = held.tile([P, 1], I32, name="run")
        nc.vector.tensor_tensor(run[:], column[:, 1:2], shifted[:, 4:5], SHIFT_LEFT)
        apart = held.tile([P, P], I32, name="apart")
        nc.vector.tensor_tensor(apart[:], column[:], base[:].to_broadcast([P, P]), XOR)

        long_place = held.tile([P, P // LONG - 1], F32, name="long_place")
        for s in LONG_STAGES:
            parts = (1 << s) // LONG
            stage_rows = eye[:, s * ANGLES // LONG : (s + 1) * ANGLES // LONG]
            nc.vector.tensor_reduce(
                long_place[:, parts - 1 : 2 * parts - 1], stage_rows.rearrange("k (h q) -> k q h", q=parts), FREE, ADD
            )
        long_spread = held.tile([P, P], F32, name="long_spread")
        nc.vector.tensor_tensor(long_spread[:], apart[:], run[:].to_broadcast([P, P]), IS_LT)

        half = P // 2
        short_spread = held.tile([P, P], F32, name="short_spread")
        nc.vector.tensor_copy(
            short_spread[:half, :].rearrange("k (h e) -> k h e", e=2),
            eye[:half, :half].unsqueeze(2).to_broadcast([half, half, 2]),
        )
        nc.vector.tensor_tensor(
            short_spread[half:, :].rearrange("k (h e) -> k h e", e=4),
            eye[half:, half::2].unsqueeze(2).to_broadcast([half, half // 2, 4]),
            eye[half:, half + 1 :: 2].unsqueeze(2).to_broadcast([half, half // 2, 4]),
            ADD,
        )
        short_place = held.tile([P, 3], F32, name="short_place")
        nc.vector.tensor_reduce(short_place[:, 0:1], eye[:, :half], FREE, ADD)
        nc.vector.tensor_reduce(short_place[:, 1:3], eye[:, half:].rearrange("k (h q) -> k q h", q=2), FREE, ADD)

        def own_angles(name, rows, place, spread):
            shape = [P, place.shape[1], rows.shape[1]]
            placed = held.tile(shape, F32, name=f"{name}_placed")
            nc.vector.tensor_tensor(
                placed[:], rows[:].unsqueeze(1).to_broadcast(shape), place[:].unsqueeze(2).to_broadcast(shape), MULT
            )
            angles = psum.tile([P, shape[1] * shape[2]], F32, name=f"{name}_angles")
            nc.tensor.matmul(angles[:], spread[:], placed[:].rearrange("k c e -> k (c e)"), start=True, stop=True)
            return angles

        long_angles = own_angles("long", long_rows, long_place, long_spread)
        for s in LONG_STAGES:
            sines(s, long_angles[:, (1 << s) - LONG : (2 << s) - LONG])
        short_angles = own_angles("short", short_rows, short_place, short_spread)
        for s in SHORT_STAGES:
            sines(s, short_angles[:, (1 << s) - SHORT : (2 << s) - SHORT])

        products = [work.tile([P, 2, PICKED], F32, name="products") for b in range(BLOCKS)]

        def rotate(b, new_bit):
            nc.vector.tensor_tensor(
                products[b][:, new_bit, :],
                windows[b][:].indirect(offsets[:]),
                first_factors[:, new_bit, :, :].rearrange("p g t -> p (g t)"),
                MULT,
            )

        def flip(b):
            sides = products[b][:].rearrange("p r (g t) -> p r t g", t=2)
            flipped_psum = psum.tile([P, 2, P], F32, name=f"flipped_psum{b}")
            for parity in range(2):
                for side in range(2):
                    nc.tensor.matmul(
                        flipped_psum[:, parity, :],
                        sides[:, parity, side, :],
                        eye[:],
                        is_transpose=not (b == 0 and parity == 1),
                        start=(side == 0),
                        stop=(side == 1),
                    )
            flipped = work.tile([P, 2, P], F32, name="flipped")
            nc.scalar.copy(flipped[:], flipped_psum[:])
            return flipped

        def stage_pair(s):
            d = 1 << s
            pair = held.tile([P, 2, 2, d], F32, name=f"pair{s}")
            nc.vector.tensor_tensor(
                pair[:],
                coef[:, :, 2 * d : 4 * d].rearrange("p b (c e) -> p b c e", c=2),
                coef[:, :, d : 2 * d].unsqueeze(1).to_broadcast([P, 2, 2, d]),
                MULT,
            )
            return pair[:].rearrange("p b c e -> p (b c e)")

        def join(name, upper, lower):
            repeats, period = upper.shape[1], upper.shape[2]
            joined = held.tile([P, repeats, period], F32, name=name)
            nc.vector.tensor_tensor(joined[:], upper, lower.unsqueeze(1).to_broadcast([P, repeats, period]), MULT)
            return joined[:].rearrange("p a e -> p (a e)")

        rotate(0, 0)
        rotate(0, 1)
        flipped_blocks = [flip(0)]
        rotate(1, 0)
        stages_1_2 = stage_pair(1)
        stages_3_4 = stage_pair(3)
        stages_5_6 = stage_pair(5)
        stages_1_4 = join("stages_1_4", stages_3_4.rearrange("p (a e) -> p a e", e=8), stages_1_2)
        rotate(1, 1)
        flipped_blocks.append(flip(1))
        stages_1_6 = [
            join(
                f"stages_1_6_{parity}",
                stages_5_6.rearrange("p (a e r) -> p r a e", e=16, r=2)[:, parity, :, :],
                stages_1_4.rearrange("p (e r) -> p r e", r=2)[:, parity, :],
            )
            for parity in range(2)
        ]
        by_parity = [
            join(
                f"matrix{parity}",
                coef[:, :, P : 2 * P].rearrange("p b (e r) -> p r b e", r=2)[:, parity, :, :],
                stages_1_6[parity],
            )
            for parity in range(2)
        ]

        out_psums = [psum.tile([P, 2, PAIRS], F32, name=f"out_psum{b}") for b in range(BLOCKS)]
        for parity in range(2):
            for b in range(BLOCKS):
                nc.tensor.matmul(out_psums[b][:, parity, :], flipped_blocks[b][:, parity, :], by_parity[parity])
        for b in range(BLOCKS):
            result = work.tile([P, PAIRS, 2], F32, name="result")
            in_order = out_psums[b][:].rearrange("p r g -> p g r")
            if b == 0:
                nc.scalar.activation(result[:], in_order, RELU)
            else:
                nc.vector.tensor_scalar_max(result[:], in_order, 0.0)
            nc.sync.dma_start(out[b * P : (b + 1) * P, :], result[:].rearrange("p g r -> p (g r)"))
